import numpy as np
import ml_dtypes


def mxq(x, axis, fmt="e4m3"):
    dtype, down = {"e4m3": (ml_dtypes.float8_e4m3fn, 7), "e5m2": (ml_dtypes.float8_e5m2, 14)}[fmt]
    v = np.moveaxis(np.asarray(x, np.float32).astype(ml_dtypes.bfloat16).astype(np.float64), axis, -1)
    blocks = v.reshape(v.shape[:-1] + (-1, 32))
    amax = np.abs(blocks).max(-1, keepdims=True)
    byte = np.maximum(np.where(amax > 0, np.frexp(amax)[1] - 1 + 127, 0) - down, 1)
    scale = np.exp2(byte - 127.0)
    codes = (blocks / scale).astype(np.float32).astype(dtype).astype(np.float64)
    return np.moveaxis((codes * scale).reshape(v.shape), -1, axis)


WIDE = False


def mx_kscale(k):
    if not WIDE:
        return np.ones(k)
    levels = np.array([10, -10, 5, -5, 0])
    a = np.random.permutation(np.resize(levels, k // 512 * 4)).reshape(k // 512, 4)
    idx = np.arange(k)
    return np.exp2(a[idx // 512, idx % 128 // 32])


BF16 = ml_dtypes.bfloat16


def bf(x):
    return np.asarray(x, np.float32).astype(BF16)


def f64(x):
    return np.asarray(x).astype(np.float64)


B, D, H, F, C = 16384, 512, 512, 128, 10


def blend_act(v):
    t = np.tanh(v)
    return np.where(v > 0, v * 0.9 + t * 0.1, t * 0.5)


def setup_inputs():
    s = mx_kscale(D)
    return {"x": bf(np.random.standard_normal((B, D)) * s),
            "W1": bf(np.random.standard_normal((D, H)) / np.sqrt(D) / s[:, None]),
            "b1": bf(np.random.standard_normal(H) * 0.3),
            "W2": bf(np.random.standard_normal((H, F)) * 1.5 / np.sqrt(H)),
            "b2": bf(np.random.standard_normal(F) * 0.3)}


def reference(x, W1, b1, W2, b2):
    h = blend_act((mxq(f64(x), 1, "e4m3") @ mxq(f64(W1), 0, "e4m3")) + f64(b1))
    return np.maximum((mxq(h, 1, "e4m3") @ mxq(f64(W2), 0, "e4m3")) + f64(b2), 0.0)

@@ -1,0 +1,175 @@
+from contextlib import ExitStack
+
+import concourse.mybir as mybir
+from concourse.masks import make_identity
+
+F32 = mybir.dt.float32
+BF16 = mybir.dt.bfloat16
+U32 = mybir.dt.uint32
+U8 = mybir.dt.uint8
+FP8X4 = mybir.dt.float8_e4m3fn_x4
+ACT = mybir.ActivationFunctionType
+ALU = mybir.AluOpType
+
+B, D, H, F = 16384, 512, 512, 128
+FLOPS = 2 * B * D * H + 2 * B * H * F
+
+P = 128
+PACK = 4
+CH = 512
+R = CH // P
+NCH = B // CH
+
+
+def tile_complexnn_pa_t_kernel(tc, x, W1, b1, W2, b2, out):
+    nc = tc.nc
+    with ExitStack() as ctx:
+        const = ctx.enter_context(tc.tile_pool(name="const", bufs=1))
+        xin = ctx.enter_context(tc.tile_pool(name="xin", bufs=3))
+        xgp = ctx.enter_context(tc.tile_pool(name="xgp", bufs=2))
+        xqp = ctx.enter_context(tc.tile_pool(name="xqp", bufs=2))
+        act = ctx.enter_context(tc.tile_pool(name="act", bufs=3))
+        hgp = ctx.enter_context(tc.tile_pool(name="hgp", bufs=2))
+        hqp = ctx.enter_context(tc.tile_pool(name="hqp", bufs=2))
+        outp = ctx.enter_context(tc.tile_pool(name="outp", bufs=3))
+        ps_x = ctx.enter_context(tc.psum_pool(name="ps_x", bufs=2))
+        ps_a = ctx.enter_context(tc.psum_pool(name="ps_a", bufs=5))
+        ps_o = ctx.enter_context(tc.psum_pool(name="ps_o", bufs=1))
+
+        def load_x(c):
+            x_sb = xin.tile([P, R, D], BF16, name="x_sb")
+            nc.sync.dma_start(
+                out=x_sb[:],
+                in_=x[c * CH : (c + 1) * CH, :].rearrange("(p r) k -> p r k", r=R),
+            )
+            return x_sb
+
+        x_first = load_x(0)
+
+        ident = const.tile([P, P], F32)
+        make_identity(nc, ident[:])
+
+        w1raw = const.tile([P, PACK, H], BF16)
+        nc.sync.dma_start(out=w1raw[:], in_=W1.rearrange("(p t) c -> p t c", t=PACK))
+        w2raw = const.tile([P, PACK, F], BF16)
+        nc.scalar.dma_start(out=w2raw[:], in_=W2.rearrange("(p t) f -> p t f", t=PACK))
+        b1raw = const.tile([P, PACK], BF16)
+        nc.scalar.dma_start(out=b1raw[:], in_=b1.rearrange("(p j) -> p j", j=PACK))
+        b2raw = const.tile([P, F], BF16)
+        nc.scalar.dma_start(out=b2raw[:], in_=b2.partition_broadcast(P))
+
+        w1g = const.tile([P, H, PACK], BF16, align_bytes=64)
+        nc.vector.tensor_copy(
+            out=w1g[:].rearrange("p (j m) t -> p j m t", j=PACK),
+            in_=w1raw[:].rearrange("p t (m j) -> p j m t", j=PACK),
+        )
+        w1q = const.tile([P, H], U32, align_bytes=64)
+        w1s = const.tile([P, H], U8, align_bytes=64)
+        nc.vector.quantize_mx(
+            out=w1q[:].bitcast(FP8X4), scales=w1s[:], in_=w1g[:].rearrange("p c t -> p (c t)")
+        )
+        w2g = const.tile([P, F, PACK], BF16, align_bytes=64)
+        nc.vector.tensor_copy(out=w2g[:], in_=w2raw[:].rearrange("p t f -> p f t"))
+        w2q = const.tile([P, F], U32, align_bytes=64)
+        w2s = const.tile([P, F], U8, align_bytes=64)
+        nc.vector.quantize_mx(
+            out=w2q[:].bitcast(FP8X4), scales=w2s[:], in_=w2g[:].rearrange("p f t -> p (f t)")
+        )
+        b1f = const.tile([P, PACK], F32)
+        nc.vector.tensor_copy(out=b1f[:], in_=b1raw[:])
+        b1s = const.tile([P, PACK], F32)
+        nc.vector.tensor_scalar_mul(out=b1s[:], in0=b1raw[:], scalar1=0.9)
+        b2f = const.tile([P, F], F32)
+        nc.vector.tensor_copy(out=b2f[:], in_=b2raw[:])
+
+        for c in range(NCH):
+            x_sb = x_first if c == 0 else load_x(c)
+            xw = x_sb[:].bitcast(F32)
+            xg = xgp.tile([P, CH * PACK], BF16, align_bytes=64)
+            xg32 = xg[:].bitcast(F32)
+            for i in range(2):
+                xt = ps_x.tile([P, 2, 2, P], F32)
+                for rr in range(2):
+                    for u in range(2):
+                        nc.tensor.transpose(
+                            xt[:, rr, u, :], xw[:, 2 * i + rr, u : D // 2 : 2], ident[:]
+                        )
+                nc.scalar.copy(
+                    out=xg32[:, 512 * i : 512 * (i + 1)].rearrange(
+                        "p (r b u) -> p r b u", r=2, u=2
+                    ),
+                    in_=xt[:].rearrange("p r u b -> p r b u"),
+                )
+            xq = xqp.tile([P, CH], U32, align_bytes=64)
+            xs = xqp.tile([P, CH], U8, align_bytes=64)
+            nc.vector.quantize_mx(out=xq[:].bitcast(FP8X4), scales=xs[:], in_=xg[:])
+
+            t = act.tile([P, PACK, CH], F32)
+            u_t = act.tile([P, PACK, CH], F32)
+            y = act.tile([P, PACK, CH], F32)
+            for j in range(PACK):
+                a = ps_a.tile([P, CH], F32)
+                nc.tensor.matmul_mx(
+                    out=a[:],
+                    lhsT=w1q[:, j * P : (j + 1) * P].bitcast(FP8X4),
+                    lhsT_scale=w1s[:, j * P : (j + 1) * P],
+                    rhs=xq[:].bitcast(FP8X4),
+                    rhs_scale=xs[:],
+                    start=True,
+                    stop=True,
+                )
+                nc.scalar.activation(
+                    out=t[:, j, :], in_=a[:], func=ACT.Tanh, bias=b1f[:, j : j + 1], scale=1.0
+                )
+                nc.vector.scalar_tensor_tensor(
+                    out=u_t[:, j, :],
+                    in0=t[:, j, :],
+                    scalar=1.0 / 9.0,
+                    in1=a[:],
+                    op0=ALU.mult,
+                    op1=ALU.add,
+                )
+                nc.scalar.activation(
+                    out=y[:, j, :],
+                    in_=u_t[:, j, :],
+                    func=ACT.Identity,
+                    bias=b1s[:, j : j + 1],
+                    scale=0.9,
+                )
+            hg = hgp.tile([P, CH, PACK], BF16, align_bytes=64)
+            nc.vector.scalar_tensor_tensor(
+                out=hg[:],
+                in0=t[:].rearrange("p j b -> p b j"),
+                scalar=0.5,
+                in1=y[:].rearrange("p j b -> p b j"),
+                op0=ALU.mult,
+                op1=ALU.max,
+            )
+            hq = hqp.tile([P, CH], U32, align_bytes=64)
+            hs = hqp.tile([P, CH], U8, align_bytes=64)
+            nc.vector.quantize_mx(
+                out=hq[:].bitcast(FP8X4), scales=hs[:], in_=hg[:].rearrange("p b j -> p (b j)")
+            )
+            o_ps = ps_o.tile([P, R, F], F32)
+            for r in range(R):
+                nc.tensor.matmul_mx(
+                    out=o_ps[:, r, :],
+                    lhsT=hq[:, r * P : (r + 1) * P].bitcast(FP8X4),
+                    lhsT_scale=hs[:, r * P : (r + 1) * P],
+                    rhs=w2q[:].bitcast(FP8X4),
+                    rhs_scale=w2s[:],
+                    start=True,
+                    stop=True,
+                )
+            o_sb = outp.tile([P, R, F], F32)
+            nc.vector.tensor_tensor(
+                out=o_sb[:],
+                in0=o_ps[:],
+                in1=b2f[:].unsqueeze(1).to_broadcast([P, R, F]),
+                op=ALU.add,
+            )
+            nc.scalar.activation(out=o_sb[:], in_=o_sb[:], func=ACT.Relu)
+            nc.sync.dma_start(
+                out=out[c * CH : (c + 1) * CH, :].rearrange("(p r) f -> p r f", r=R),
+                in_=o_sb[:],
+            )

@@ -40,7 +40,7 @@ def tile_complexnn_pa_t_kernel(tc, x, W1, b1, W2, b2, out):
             x_sb = xin.tile([P, R, D], BF16, name="x_sb")
             nc.sync.dma_start(
                 out=x_sb[:],
-                in_=x[c * CH : (c + 1) * CH, :].rearrange("(p r) k -> p r k", r=R),
+                in_=x[c * CH : (c + 1) * CH, :].rearrange("(r p) k -> p r k", p=P),
             )
             return x_sb
 
@@ -104,9 +104,9 @@ def tile_complexnn_pa_t_kernel(tc, x, W1, b1, W2, b2, out):
             xs = xqp.tile([P, CH], U8, align_bytes=64)
             nc.vector.quantize_mx(out=xq[:].bitcast(FP8X4), scales=xs[:], in_=xg[:])
 
-            t = act.tile([P, PACK, CH], F32)
-            u_t = act.tile([P, PACK, CH], F32)
-            y = act.tile([P, PACK, CH], F32)
+            t = act.tile([P, CH // 4, PACK, 4], F32)
+            u_t = act.tile([P, CH // 4, PACK, 4], F32)
+            y = act.tile([P, CH // 4, PACK, 4], F32)
             for j in range(PACK):
                 a = ps_a.tile([P, CH], F32)
                 nc.tensor.matmul_mx(
@@ -118,37 +118,38 @@ def tile_complexnn_pa_t_kernel(tc, x, W1, b1, W2, b2, out):
                     start=True,
                     stop=True,
                 )
+                a_v = a[:].rearrange("p (c i) -> p c i", i=4)
                 nc.scalar.activation(
-                    out=t[:, j, :], in_=a[:], func=ACT.Tanh, bias=b1f[:, j : j + 1], scale=1.0
+                    out=t[:, :, j, :], in_=a_v, func=ACT.Tanh, bias=b1f[:, j : j + 1], scale=1.0
                 )
                 nc.vector.scalar_tensor_tensor(
-                    out=u_t[:, j, :],
-                    in0=t[:, j, :],
+                    out=u_t[:, :, j, :],
+                    in0=t[:, :, j, :],
                     scalar=1.0 / 9.0,
-                    in1=a[:],
+                    in1=a_v,
                     op0=ALU.mult,
                     op1=ALU.add,
                 )
                 nc.scalar.activation(
-                    out=y[:, j, :],
-                    in_=u_t[:, j, :],
+                    out=y[:, :, j, :],
+                    in_=u_t[:, :, j, :],
                     func=ACT.Identity,
                     bias=b1s[:, j : j + 1],
                     scale=0.9,
                 )
-            hg = hgp.tile([P, CH, PACK], BF16, align_bytes=64)
+            hg = hgp.tile([P, 4, CH // 4, PACK], BF16, align_bytes=64)
             nc.vector.scalar_tensor_tensor(
-                out=hg[:],
-                in0=t[:].rearrange("p j b -> p b j"),
+                out=hg[:].rearrange("p i c j -> p (c j) i"),
+                in0=t[:].rearrange("p c j i -> p (c j) i"),
                 scalar=0.5,
-                in1=y[:].rearrange("p j b -> p b j"),
+                in1=y[:].rearrange("p c j i -> p (c j) i"),
                 op0=ALU.mult,
                 op1=ALU.max,
             )
             hq = hqp.tile([P, CH], U32, align_bytes=64)
             hs = hqp.tile([P, CH], U8, align_bytes=64)
             nc.vector.quantize_mx(
-                out=hq[:].bitcast(FP8X4), scales=hs[:], in_=hg[:].rearrange("p b j -> p (b j)")
+                out=hq[:].bitcast(FP8X4), scales=hs[:], in_=hg[:].rearrange("p i c j -> p (i c j)")
             )
             o_ps = ps_o.tile([P, R, F], F32)
             for r in range(R):

@@ -25,152 +25,246 @@ def tile_complexnn_pa_t_kernel(tc, x, W1, b1, W2, b2, out):
     nc = tc.nc
     with ExitStack() as ctx:
         const = ctx.enter_context(tc.tile_pool(name="const", bufs=1))
-        xin = ctx.enter_context(tc.tile_pool(name="xin", bufs=3))
+        xin = ctx.enter_context(tc.tile_pool(name="xin", bufs=4))
         xgp = ctx.enter_context(tc.tile_pool(name="xgp", bufs=2))
         xqp = ctx.enter_context(tc.tile_pool(name="xqp", bufs=2))
         act = ctx.enter_context(tc.tile_pool(name="act", bufs=3))
         hgp = ctx.enter_context(tc.tile_pool(name="hgp", bufs=2))
         hqp = ctx.enter_context(tc.tile_pool(name="hqp", bufs=2))
-        outp = ctx.enter_context(tc.tile_pool(name="outp", bufs=3))
+        outp = ctx.enter_context(tc.tile_pool(name="outp", bufs=4))
         ps_x = ctx.enter_context(tc.psum_pool(name="ps_x", bufs=2))
         ps_a = ctx.enter_context(tc.psum_pool(name="ps_a", bufs=5))
         ps_o = ctx.enter_context(tc.psum_pool(name="ps_o", bufs=1))
+        ctx.enter_context(tc.manual_schedule())
 
-        def load_x(c):
+        live = {}
+
+        def ok(c):
+            return 0 <= c < NCH
+
+        w1raw = const.tile([P, PACK, H], BF16)
+        nc.scalar.dma_start(out=w1raw[:], in_=W1.rearrange("(p t) c -> p t c", t=PACK))
+        b1raw = const.tile([P, PACK], BF16)
+        nc.scalar.dma_start(out=b1raw[:], in_=b1.rearrange("(p j) -> p j", j=PACK))
+        w2raw = const.tile([P, PACK, F], BF16)
+        nc.scalar.dma_start(out=w2raw[:], in_=W2.rearrange("(p t) f -> p t f", t=PACK))
+        b2raw = const.tile([P, F], BF16)
+        ident = const.tile([P, P], F32)
+        make_identity(nc, ident[:])
+
+        w1g = const.tile([P, H, PACK], BF16, align_bytes=64)
+        w1q = const.tile([P, H], U32, align_bytes=64)
+        w1s = const.tile([P, H], U8, align_bytes=64)
+        w2g = const.tile([P, F, PACK], BF16, align_bytes=64)
+        w2q = const.tile([P, F], U32, align_bytes=64)
+        w2s = const.tile([P, F], U8, align_bytes=64)
+        b1f = const.tile([P, PACK], F32)
+        b1s = const.tile([P, PACK], F32)
+        b2f = const.tile([P, F], F32)
+
+        def w1_group(j):
+            nc.vector.tensor_copy(
+                out=w1g[:, j * P : (j + 1) * P, :],
+                in_=w1raw[:].rearrange("p t (m j) -> p j m t", j=PACK)[:, j],
+            )
+
+        def w1_quant(j):
+            nc.vector.quantize_mx(
+                out=w1q[:, j * P : (j + 1) * P].bitcast(FP8X4),
+                scales=w1s[:, j * P : (j + 1) * P],
+                in_=w1g[:, j * P : (j + 1) * P, :].rearrange("p m t -> p (m t)"),
+            )
+
+        def w2_prep():
+            nc.vector.tensor_copy(out=w2g[:], in_=w2raw[:].rearrange("p t f -> p f t"))
+            nc.vector.tensor_copy(out=b2f[:], in_=b2raw[:])
+            nc.vector.quantize_mx(
+                out=w2q[:].bitcast(FP8X4),
+                scales=w2s[:],
+                in_=w2g[:].rearrange("p f t -> p (f t)"),
+            )
+
+        def load(c):
             x_sb = xin.tile([P, R, D], BF16, name="x_sb")
             nc.sync.dma_start(
                 out=x_sb[:],
                 in_=x[c * CH : (c + 1) * CH, :].rearrange("(r p) k -> p r k", p=P),
             )
-            return x_sb
+            live["x", c] = x_sb
 
-        x_first = load_x(0)
-
-        ident = const.tile([P, P], F32)
-        make_identity(nc, ident[:])
-
-        w1raw = const.tile([P, PACK, H], BF16)
-        nc.sync.dma_start(out=w1raw[:], in_=W1.rearrange("(p t) c -> p t c", t=PACK))
-        w2raw = const.tile([P, PACK, F], BF16)
-        nc.scalar.dma_start(out=w2raw[:], in_=W2.rearrange("(p t) f -> p t f", t=PACK))
-        b1raw = const.tile([P, PACK], BF16)
-        nc.scalar.dma_start(out=b1raw[:], in_=b1.rearrange("(p j) -> p j", j=PACK))
-        b2raw = const.tile([P, F], BF16)
-        nc.scalar.dma_start(out=b2raw[:], in_=b2.partition_broadcast(P))
-
-        w1g = const.tile([P, H, PACK], BF16, align_bytes=64)
-        nc.vector.tensor_copy(
-            out=w1g[:].rearrange("p (j m) t -> p j m t", j=PACK),
-            in_=w1raw[:].rearrange("p t (m j) -> p j m t", j=PACK),
-        )
-        w1q = const.tile([P, H], U32, align_bytes=64)
-        w1s = const.tile([P, H], U8, align_bytes=64)
-        nc.vector.quantize_mx(
-            out=w1q[:].bitcast(FP8X4), scales=w1s[:], in_=w1g[:].rearrange("p c t -> p (c t)")
-        )
-        w2g = const.tile([P, F, PACK], BF16, align_bytes=64)
-        nc.vector.tensor_copy(out=w2g[:], in_=w2raw[:].rearrange("p t f -> p f t"))
-        w2q = const.tile([P, F], U32, align_bytes=64)
-        w2s = const.tile([P, F], U8, align_bytes=64)
-        nc.vector.quantize_mx(
-            out=w2q[:].bitcast(FP8X4), scales=w2s[:], in_=w2g[:].rearrange("p f t -> p (f t)")
-        )
-        b1f = const.tile([P, PACK], F32)
-        nc.vector.tensor_copy(out=b1f[:], in_=b1raw[:])
-        b1s = const.tile([P, PACK], F32)
-        nc.vector.tensor_scalar_mul(out=b1s[:], in0=b1raw[:], scalar1=0.9)
-        b2f = const.tile([P, F], F32)
-        nc.vector.tensor_copy(out=b2f[:], in_=b2raw[:])
-
-        for c in range(NCH):
-            x_sb = x_first if c == 0 else load_x(c)
-            xw = x_sb[:].bitcast(F32)
-            xg = xgp.tile([P, CH * PACK], BF16, align_bytes=64)
-            xg32 = xg[:].bitcast(F32)
+        def transposes(c):
+            xw = live["x", c][:].bitcast(F32)
             for i in range(2):
-                xt = ps_x.tile([P, 2, 2, P], F32)
+                xt = ps_x.tile([P, 2, 2, P], F32, name="xt")
                 for rr in range(2):
                     for u in range(2):
                         nc.tensor.transpose(
                             xt[:, rr, u, :], xw[:, 2 * i + rr, u : D // 2 : 2], ident[:]
                         )
+                live["xt", c, i] = xt
+
+        def evacuate(c):
+            xg = xgp.tile([P, CH * PACK], BF16, align_bytes=64, name="xg")
+            xg32 = xg[:].bitcast(F32)
+            for i in range(2):
                 nc.scalar.copy(
                     out=xg32[:, 512 * i : 512 * (i + 1)].rearrange(
                         "p (r b u) -> p r b u", r=2, u=2
                     ),
-                    in_=xt[:].rearrange("p r u b -> p r b u"),
+                    in_=live["xt", c, i][:].rearrange("p r u b -> p r b u"),
                 )
-            xq = xqp.tile([P, CH], U32, align_bytes=64)
-            xs = xqp.tile([P, CH], U8, align_bytes=64)
-            nc.vector.quantize_mx(out=xq[:].bitcast(FP8X4), scales=xs[:], in_=xg[:])
+            live["xg", c] = xg
 
-            t = act.tile([P, CH // 4, PACK, 4], F32)
-            u_t = act.tile([P, CH // 4, PACK, 4], F32)
-            y = act.tile([P, CH // 4, PACK, 4], F32)
-            for j in range(PACK):
-                a = ps_a.tile([P, CH], F32)
-                nc.tensor.matmul_mx(
-                    out=a[:],
-                    lhsT=w1q[:, j * P : (j + 1) * P].bitcast(FP8X4),
-                    lhsT_scale=w1s[:, j * P : (j + 1) * P],
-                    rhs=xq[:].bitcast(FP8X4),
-                    rhs_scale=xs[:],
-                    start=True,
-                    stop=True,
-                )
-                a_v = a[:].rearrange("p (c i) -> p c i", i=4)
-                nc.scalar.activation(
-                    out=t[:, :, j, :], in_=a_v, func=ACT.Tanh, bias=b1f[:, j : j + 1], scale=1.0
-                )
-                nc.vector.scalar_tensor_tensor(
-                    out=u_t[:, :, j, :],
-                    in0=t[:, :, j, :],
-                    scalar=1.0 / 9.0,
-                    in1=a_v,
-                    op0=ALU.mult,
-                    op1=ALU.add,
-                )
-                nc.scalar.activation(
-                    out=y[:, :, j, :],
-                    in_=u_t[:, :, j, :],
-                    func=ACT.Identity,
-                    bias=b1s[:, j : j + 1],
-                    scale=0.9,
-                )
-            hg = hgp.tile([P, 4, CH // 4, PACK], BF16, align_bytes=64)
+        def quant_x(c):
+            xq = xqp.tile([P, CH], U32, align_bytes=64, name="xq")
+            xs = xqp.tile([P, CH], U8, align_bytes=64, name="xs")
+            nc.vector.quantize_mx(out=xq[:].bitcast(FP8X4), scales=xs[:], in_=live["xg", c][:])
+            live["xq", c] = xq
+            live["xs", c] = xs
+
+        def layer1(c, j):
+            a = ps_a.tile([P, CH], F32, name="a")
+            nc.tensor.matmul_mx(
+                out=a[:],
+                lhsT=w1q[:, j * P : (j + 1) * P].bitcast(FP8X4),
+                lhsT_scale=w1s[:, j * P : (j + 1) * P],
+                rhs=live["xq", c][:].bitcast(FP8X4),
+                rhs_scale=live["xs", c][:],
+                start=True,
+                stop=True,
+            )
+            live["a", c, j] = a
+
+        def tanh(c, j):
+            if j == 0:
+                live["t", c] = act.tile([P, CH // 4, PACK, 4], F32, name="t")
+                live["u", c] = act.tile([P, CH // 4, PACK, 4], F32, name="u_t")
+                live["y", c] = act.tile([P, CH // 4, PACK, 4], F32, name="y")
+            nc.scalar.activation(
+                out=live["t", c][:, :, j, :],
+                in_=live["a", c, j][:].rearrange("p (c i) -> p c i", i=4),
+                func=ACT.Tanh,
+                bias=b1f[:, j : j + 1],
+                scale=1.0,
+            )
+
+        def mix(c, j):
+            nc.vector.scalar_tensor_tensor(
+                out=live["u", c][:, :, j, :],
+                in0=live["t", c][:, :, j, :],
+                scalar=1.0 / 9.0,
+                in1=live["a", c, j][:].rearrange("p (c i) -> p c i", i=4),
+                op0=ALU.mult,
+                op1=ALU.add,
+            )
+
+        def affine(c, j):
+            nc.scalar.activation(
+                out=live["y", c][:, :, j, :],
+                in_=live["u", c][:, :, j, :],
+                func=ACT.Identity,
+                bias=b1s[:, j : j + 1],
+                scale=0.9,
+            )
+
+        def blend_max(c):
+            hg = hgp.tile([P, 4, CH // 4, PACK], BF16, align_bytes=64, name="hg")
             nc.vector.scalar_tensor_tensor(
                 out=hg[:].rearrange("p i c j -> p (c j) i"),
-                in0=t[:].rearrange("p c j i -> p (c j) i"),
+                in0=live["t", c][:].rearrange("p c j i -> p (c j) i"),
                 scalar=0.5,
-                in1=y[:].rearrange("p c j i -> p (c j) i"),
+                in1=live["y", c][:].rearrange("p c j i -> p (c j) i"),
                 op0=ALU.mult,
                 op1=ALU.max,
             )
-            hq = hqp.tile([P, CH], U32, align_bytes=64)
-            hs = hqp.tile([P, CH], U8, align_bytes=64)
+            live["hg", c] = hg
+
+        def quant_h(c):
+            hq = hqp.tile([P, CH], U32, align_bytes=64, name="hq")
+            hs = hqp.tile([P, CH], U8, align_bytes=64, name="hs")
             nc.vector.quantize_mx(
-                out=hq[:].bitcast(FP8X4), scales=hs[:], in_=hg[:].rearrange("p i c j -> p (i c j)")
+                out=hq[:].bitcast(FP8X4),
+                scales=hs[:],
+                in_=live["hg", c][:].rearrange("p i c j -> p (i c j)"),
             )
-            o_ps = ps_o.tile([P, R, F], F32)
+            live["hq", c] = hq
+            live["hs", c] = hs
+
+        def layer2(c):
+            o_ps = ps_o.tile([P, R, F], F32, name="o_ps")
             for r in range(R):
                 nc.tensor.matmul_mx(
                     out=o_ps[:, r, :],
-                    lhsT=hq[:, r * P : (r + 1) * P].bitcast(FP8X4),
-                    lhsT_scale=hs[:, r * P : (r + 1) * P],
+                    lhsT=live["hq", c][:, r * P : (r + 1) * P].bitcast(FP8X4),
+                    lhsT_scale=live["hs", c][:, r * P : (r + 1) * P],
                     rhs=w2q[:].bitcast(FP8X4),
                     rhs_scale=w2s[:],
                     start=True,
                     stop=True,
                 )
-            o_sb = outp.tile([P, R, F], F32)
+            live["o_ps", c] = o_ps
+
+        def add_b2(c):
+            o_sb = outp.tile([P, R, F], F32, name="o_sb")
             nc.vector.tensor_tensor(
                 out=o_sb[:],
-                in0=o_ps[:],
+                in0=live["o_ps", c][:],
                 in1=b2f[:].unsqueeze(1).to_broadcast([P, R, F]),
                 op=ALU.add,
             )
+            live["o", c] = o_sb
+
+        def relu_store(c):
+            o_sb = live["o", c]
             nc.scalar.activation(out=o_sb[:], in_=o_sb[:], func=ACT.Relu)
             nc.sync.dma_start(
                 out=out[c * CH : (c + 1) * CH, :].rearrange("(p r) f -> p r f", r=R),
                 in_=o_sb[:],
             )
+
+        for s in range(-3, NCH + 3):
+            if ok(s + 3):
+                load(s + 3)
+            if s == -1:
+                nc.sync.dma_start(out=b2raw[:], in_=b2.partition_broadcast(P))
+            if s == -3:
+                w1_group(0)
+                w1_group(1)
+                w1_quant(0)
+                w1_quant(1)
+                nc.vector.tensor_copy(out=b1f[:], in_=b1raw[:])
+                nc.vector.tensor_scalar_mul(out=b1s[:], in0=b1raw[:], scalar1=0.9)
+            if ok(s - 2):
+                layer2(s - 2)
+            if ok(s + 2):
+                transposes(s + 2)
+            for j in range(PACK):
+                if ok(s):
+                    tanh(s, j)
+                    mix(s, j)
+                if j == 1 and ok(s + 1):
+                    quant_x(s + 1)
+                    layer1(s + 1, 0)
+                    layer1(s + 1, 1)
+                    if s + 1 == 0:
+                        w1_group(2)
+                        w1_group(3)
+                        w1_quant(2)
+                        w1_quant(3)
+                if j >= 2 and ok(s + 1):
+                    layer1(s + 1, j)
+            if s == 0:
+                w2_prep()
+            for j in range(PACK):
+                if ok(s):
+                    affine(s, j)
+            if ok(s + 2):
+                evacuate(s + 2)
+            if ok(s - 1):
+                blend_max(s - 1)
+            if ok(s - 2):
+                add_b2(s - 2)
+            if ok(s - 1):
+                quant_h(s - 1)
+            if ok(s - 3):
+                relu_store(s - 3)

@@ -25,7 +25,7 @@ def tile_complexnn_pa_t_kernel(tc, x, W1, b1, W2, b2, out):
     nc = tc.nc
     with ExitStack() as ctx:
         const = ctx.enter_context(tc.tile_pool(name="const", bufs=1))
-        xin = ctx.enter_context(tc.tile_pool(name="xin", bufs=4))
+        xin = ctx.enter_context(tc.tile_pool(name="xin", bufs=5))
         xgp = ctx.enter_context(tc.tile_pool(name="xgp", bufs=2))
         xqp = ctx.enter_context(tc.tile_pool(name="xqp", bufs=2))
         act = ctx.enter_context(tc.tile_pool(name="act", bufs=3))
@@ -33,8 +33,9 @@ def tile_complexnn_pa_t_kernel(tc, x, W1, b1, W2, b2, out):
         hqp = ctx.enter_context(tc.tile_pool(name="hqp", bufs=2))
         outp = ctx.enter_context(tc.tile_pool(name="outp", bufs=4))
         ps_x = ctx.enter_context(tc.psum_pool(name="ps_x", bufs=2))
-        ps_a = ctx.enter_context(tc.psum_pool(name="ps_a", bufs=5))
+        ps_a = ctx.enter_context(tc.psum_pool(name="ps_a", bufs=4))
         ps_o = ctx.enter_context(tc.psum_pool(name="ps_o", bufs=1))
+        ps_t = ctx.enter_context(tc.psum_pool(name="ps_t", bufs=1))
         ctx.enter_context(tc.manual_schedule())
 
         live = {}
@@ -48,7 +49,8 @@ def tile_complexnn_pa_t_kernel(tc, x, W1, b1, W2, b2, out):
         nc.scalar.dma_start(out=b1raw[:], in_=b1.rearrange("(p j) -> p j", j=PACK))
         w2raw = const.tile([P, PACK, F], BF16)
         nc.scalar.dma_start(out=w2raw[:], in_=W2.rearrange("(p t) f -> p t f", t=PACK))
-        b2raw = const.tile([P, F], BF16)
+        b2raw = const.tile([P, 1], BF16)
+        nc.scalar.dma_start(out=b2raw[:], in_=b2.rearrange("(p o) -> p o", o=1))
         ident = const.tile([P, P], F32)
         make_identity(nc, ident[:])
 
@@ -60,7 +62,7 @@ def tile_complexnn_pa_t_kernel(tc, x, W1, b1, W2, b2, out):
         w2s = const.tile([P, F], U8, align_bytes=64)
         b1f = const.tile([P, PACK], F32)
         b1s = const.tile([P, PACK], F32)
-        b2f = const.tile([P, F], F32)
+        b2f = const.tile([P, 1], F32)
 
         def w1_group(j):
             nc.vector.tensor_copy(
@@ -159,13 +161,23 @@ def tile_complexnn_pa_t_kernel(tc, x, W1, b1, W2, b2, out):
             )
 
         def affine(c, j):
-            nc.scalar.activation(
-                out=live["y", c][:, :, j, :],
-                in_=live["u", c][:, :, j, :],
-                func=ACT.Identity,
-                bias=b1s[:, j : j + 1],
-                scale=0.9,
-            )
+            if j < 2:
+                nc.gpsimd.tensor_scalar(
+                    out=live["y", c][:, :, j, :],
+                    in0=live["u", c][:, :, j, :],
+                    scalar1=0.9,
+                    scalar2=b1s[:, j : j + 1],
+                    op0=ALU.mult,
+                    op1=ALU.add,
+                )
+            else:
+                nc.scalar.activation(
+                    out=live["y", c][:, :, j, :],
+                    in_=live["u", c][:, :, j, :],
+                    func=ACT.Identity,
+                    bias=b1s[:, j : j + 1],
+                    scale=0.9,
+                )
 
         def blend_max(c):
             hg = hgp.tile([P, 4, CH // 4, PACK], BF16, align_bytes=64, name="hg")
@@ -191,43 +203,43 @@ def tile_complexnn_pa_t_kernel(tc, x, W1, b1, W2, b2, out):
             live["hs", c] = hs
 
         def layer2(c):
-            o_ps = ps_o.tile([P, R, F], F32, name="o_ps")
-            for r in range(R):
-                nc.tensor.matmul_mx(
-                    out=o_ps[:, r, :],
-                    lhsT=live["hq", c][:, r * P : (r + 1) * P].bitcast(FP8X4),
-                    lhsT_scale=live["hs", c][:, r * P : (r + 1) * P],
-                    rhs=w2q[:].bitcast(FP8X4),
-                    rhs_scale=w2s[:],
-                    start=True,
-                    stop=True,
-                )
+            o_ps = ps_o.tile([P, CH], F32, name="o_ps")
+            nc.tensor.matmul_mx(
+                out=o_ps[:],
+                lhsT=w2q[:].bitcast(FP8X4),
+                lhsT_scale=w2s[:],
+                rhs=live["hq", c][:].bitcast(FP8X4),
+                rhs_scale=live["hs", c][:],
+                start=True,
+                stop=True,
+            )
             live["o_ps", c] = o_ps
 
-        def add_b2(c):
-            o_sb = outp.tile([P, R, F], F32, name="o_sb")
-            nc.vector.tensor_tensor(
-                out=o_sb[:],
-                in0=live["o_ps", c][:],
-                in1=b2f[:].unsqueeze(1).to_broadcast([P, R, F]),
-                op=ALU.add,
+        def bias_relu(c):
+            o_t = outp.tile([P, CH], F32, name="o_t")
+            nc.scalar.activation(
+                out=o_t[:], in_=live["o_ps", c][:], func=ACT.Relu, bias=b2f[:, 0:1], scale=1.0
             )
-            live["o", c] = o_sb
+            live["o_t", c] = o_t
 
-        def relu_store(c):
-            o_sb = live["o", c]
-            nc.scalar.activation(out=o_sb[:], in_=o_sb[:], func=ACT.Relu)
+        def turn_back(c):
+            ot = ps_t.tile([P, R, F], F32, name="ot")
+            for r in range(R):
+                nc.tensor.transpose(ot[:, r, :], live["o_t", c][:, r * P : (r + 1) * P], ident[:])
+            live["ot", c] = ot
+
+        def store(c):
+            o_sb = outp.tile([P, R, F], F32, name="o_sb")
+            nc.scalar.copy(out=o_sb[:], in_=live["ot", c][:])
             nc.sync.dma_start(
                 out=out[c * CH : (c + 1) * CH, :].rearrange("(p r) f -> p r f", r=R),
                 in_=o_sb[:],
             )
 
-        for s in range(-3, NCH + 3):
-            if ok(s + 3):
-                load(s + 3)
-            if s == -1:
-                nc.sync.dma_start(out=b2raw[:], in_=b2.partition_broadcast(P))
-            if s == -3:
+        for s in range(-4, NCH + 4):
+            if ok(s + 4):
+                load(s + 4)
+            if s == -4:
                 w1_group(0)
                 w1_group(1)
                 w1_quant(0)
@@ -236,35 +248,38 @@ def tile_complexnn_pa_t_kernel(tc, x, W1, b1, W2, b2, out):
                 nc.vector.tensor_scalar_mul(out=b1s[:], in0=b1raw[:], scalar1=0.9)
             if ok(s - 2):
                 layer2(s - 2)
-            if ok(s + 2):
-                transposes(s + 2)
+            if ok(s + 3):
+                transposes(s + 3)
             for j in range(PACK):
                 if ok(s):
                     tanh(s, j)
+            for j in range(PACK):
+                if ok(s):
                     mix(s, j)
-                if j == 1 and ok(s + 1):
-                    quant_x(s + 1)
-                    layer1(s + 1, 0)
-                    layer1(s + 1, 1)
-                    if s + 1 == 0:
-                        w1_group(2)
-                        w1_group(3)
-                        w1_quant(2)
-                        w1_quant(3)
-                if j >= 2 and ok(s + 1):
+                    if j < 2:
+                        affine(s, j)
+                if ok(s + 1):
                     layer1(s + 1, j)
             if s == 0:
                 w2_prep()
-            for j in range(PACK):
+            if ok(s - 3):
+                store(s - 3)
+            for j in range(2, PACK):
                 if ok(s):
                     affine(s, j)
-            if ok(s + 2):
-                evacuate(s + 2)
+            if ok(s + 3):
+                evacuate(s + 3)
+            if ok(s - 2):
+                bias_relu(s - 2)
+                turn_back(s - 2)
             if ok(s - 1):
                 blend_max(s - 1)
-            if ok(s - 2):
-                add_b2(s - 2)
+            if ok(s + 2):
+                quant_x(s + 2)
+                if s + 2 == 0:
+                    w1_group(2)
+                    w1_group(3)
+                    w1_quant(2)
+                    w1_quant(3)
             if ok(s - 1):
                 quant_h(s - 1)
-            if ok(s - 3):
-                relu_store(s - 3)

@@ -44,7 +44,7 @@ def tile_complexnn_pa_t_kernel(tc, x, W1, b1, W2, b2, out):
             return 0 <= c < NCH
 
         w1raw = const.tile([P, PACK, H], BF16)
-        nc.scalar.dma_start(out=w1raw[:], in_=W1.rearrange("(p t) c -> p t c", t=PACK))
+        nc.sync.dma_start(out=w1raw[:], in_=W1.rearrange("(p t) c -> p t c", t=PACK))
         b1raw = const.tile([P, PACK], BF16)
         nc.scalar.dma_start(out=b1raw[:], in_=b1.rearrange("(p j) -> p j", j=PACK))
         w2raw = const.tile([P, PACK, F], BF16)
@@ -141,7 +141,7 @@ def tile_complexnn_pa_t_kernel(tc, x, W1, b1, W2, b2, out):
             if j == 0:
                 live["t", c] = act.tile([P, CH // 4, PACK, 4], F32, name="t")
                 live["u", c] = act.tile([P, CH // 4, PACK, 4], F32, name="u_t")
-                live["y", c] = act.tile([P, CH // 4, PACK, 4], F32, name="y")
+                live["y", c] = act.tile([P, CH // 4, PACK, 8], F32, name="y")
             nc.scalar.activation(
                 out=live["t", c][:, :, j, :],
                 in_=live["a", c, j][:].rearrange("p (c i) -> p c i", i=4),
@@ -161,9 +161,9 @@ def tile_complexnn_pa_t_kernel(tc, x, W1, b1, W2, b2, out):
             )
 
         def affine(c, j):
-            if j < 2:
+            if j != 2:
                 nc.gpsimd.tensor_scalar(
-                    out=live["y", c][:, :, j, :],
+                    out=live["y", c][:, :, j, 0:4],
                     in0=live["u", c][:, :, j, :],
                     scalar1=0.9,
                     scalar2=b1s[:, j : j + 1],
@@ -172,7 +172,7 @@ def tile_complexnn_pa_t_kernel(tc, x, W1, b1, W2, b2, out):
                 )
             else:
                 nc.scalar.activation(
-                    out=live["y", c][:, :, j, :],
+                    out=live["y", c][:, :, j, 0:4],
                     in_=live["u", c][:, :, j, :],
                     func=ACT.Identity,
                     bias=b1s[:, j : j + 1],
@@ -185,7 +185,7 @@ def tile_complexnn_pa_t_kernel(tc, x, W1, b1, W2, b2, out):
                 out=hg[:].rearrange("p i c j -> p (c j) i"),
                 in0=live["t", c][:].rearrange("p c j i -> p (c j) i"),
                 scalar=0.5,
-                in1=live["y", c][:].rearrange("p c j i -> p (c j) i"),
+                in1=live["y", c][:, :, :, 0:4].rearrange("p c j i -> p (c j) i"),
                 op0=ALU.mult,
                 op1=ALU.max,
             )
@@ -243,9 +243,13 @@ def tile_complexnn_pa_t_kernel(tc, x, W1, b1, W2, b2, out):
                 w1_group(0)
                 w1_group(1)
                 w1_quant(0)
+                w1_group(2)
                 w1_quant(1)
+                w1_group(3)
+                w1_quant(2)
                 nc.vector.tensor_copy(out=b1f[:], in_=b1raw[:])
                 nc.vector.tensor_scalar_mul(out=b1s[:], in0=b1raw[:], scalar1=0.9)
+                w1_quant(3)
             if ok(s - 2):
                 layer2(s - 2)
             if ok(s + 3):
@@ -256,7 +260,7 @@ def tile_complexnn_pa_t_kernel(tc, x, W1, b1, W2, b2, out):
             for j in range(PACK):
                 if ok(s):
                     mix(s, j)
-                    if j < 2:
+                    if j != 2:
                         affine(s, j)
                 if ok(s + 1):
                     layer1(s + 1, j)
@@ -264,9 +268,8 @@ def tile_complexnn_pa_t_kernel(tc, x, W1, b1, W2, b2, out):
                 w2_prep()
             if ok(s - 3):
                 store(s - 3)
-            for j in range(2, PACK):
-                if ok(s):
-                    affine(s, j)
+            if ok(s):
+                affine(s, 2)
             if ok(s + 3):
                 evacuate(s + 3)
             if ok(s - 2):
@@ -276,10 +279,5 @@ def tile_complexnn_pa_t_kernel(tc, x, W1, b1, W2, b2, out):
                 blend_max(s - 1)
             if ok(s + 2):
                 quant_x(s + 2)
-                if s + 2 == 0:
-                    w1_group(2)
-                    w1_group(3)
-                    w1_quant(2)
-                    w1_quant(3)
             if ok(s - 1):
                 quant_h(s - 1)

@@ -44,7 +44,11 @@ def tile_complexnn_pa_t_kernel(tc, x, W1, b1, W2, b2, out):
             return 0 <= c < NCH
 
         w1raw = const.tile([P, PACK, H], BF16)
-        nc.sync.dma_start(out=w1raw[:], in_=W1.rearrange("(p t) c -> p t c", t=PACK))
+        for u in range(2):
+            nc.sync.dma_start(
+                out=w1raw[:, 2 * u : 2 * u + 2, :],
+                in_=W1[256 * u : 256 * (u + 1), :].rearrange("(p e) c -> p e c", e=2),
+            )
         b1raw = const.tile([P, PACK], BF16)
         nc.scalar.dma_start(out=b1raw[:], in_=b1.rearrange("(p j) -> p j", j=PACK))
         w2raw = const.tile([P, PACK, F], BF16)
@@ -101,7 +105,7 @@ def tile_complexnn_pa_t_kernel(tc, x, W1, b1, W2, b2, out):
                 for rr in range(2):
                     for u in range(2):
                         nc.tensor.transpose(
-                            xt[:, rr, u, :], xw[:, 2 * i + rr, u : D // 2 : 2], ident[:]
+                            xt[:, rr, u, :], xw[:, 2 * i + rr, u * P : (u + 1) * P], ident[:]
                         )
                 live["xt", c, i] = xt
 
@@ -140,7 +144,7 @@ def tile_complexnn_pa_t_kernel(tc, x, W1, b1, W2, b2, out):
         def tanh(c, j):
             if j == 0:
                 live["t", c] = act.tile([P, CH // 4, PACK, 4], F32, name="t")
-                live["u", c] = act.tile([P, CH // 4, PACK, 4], F32, name="u_t")
+                live["u", c] = act.tile([P, PACK, CH], F32, name="u_t")
                 live["y", c] = act.tile([P, CH // 4, PACK, 8], F32, name="y")
             nc.scalar.activation(
                 out=live["t", c][:, :, j, :],
@@ -152,7 +156,7 @@ def tile_complexnn_pa_t_kernel(tc, x, W1, b1, W2, b2, out):
 
         def mix(c, j):
             nc.vector.scalar_tensor_tensor(
-                out=live["u", c][:, :, j, :],
+                out=live["u", c][:, j, :].rearrange("p (c i) -> p c i", i=4),
                 in0=live["t", c][:, :, j, :],
                 scalar=1.0 / 9.0,
                 in1=live["a", c, j][:].rearrange("p (c i) -> p c i", i=4),
@@ -164,7 +168,7 @@ def tile_complexnn_pa_t_kernel(tc, x, W1, b1, W2, b2, out):
             if j != 2:
                 nc.gpsimd.tensor_scalar(
                     out=live["y", c][:, :, j, 0:4],
-                    in0=live["u", c][:, :, j, :],
+                    in0=live["u", c][:, j, :].rearrange("p (c i) -> p c i", i=4),
                     scalar1=0.9,
                     scalar2=b1s[:, j : j + 1],
                     op0=ALU.mult,
@@ -173,7 +177,7 @@ def tile_complexnn_pa_t_kernel(tc, x, W1, b1, W2, b2, out):
             else:
                 nc.scalar.activation(
                     out=live["y", c][:, :, j, 0:4],
-                    in_=live["u", c][:, :, j, :],
+                    in_=live["u", c][:, j, :].rearrange("p (c i) -> p c i", i=4),
                     func=ACT.Identity,
                     bias=b1s[:, j : j + 1],
                     scale=0.9,
@@ -252,8 +256,6 @@ def tile_complexnn_pa_t_kernel(tc, x, W1, b1, W2, b2, out):
                 w1_quant(3)
             if ok(s - 2):
                 layer2(s - 2)
-            if ok(s + 3):
-                transposes(s + 3)
             for j in range(PACK):
                 if ok(s):
                     tanh(s, j)
@@ -270,11 +272,14 @@ def tile_complexnn_pa_t_kernel(tc, x, W1, b1, W2, b2, out):
                 store(s - 3)
             if ok(s):
                 affine(s, 2)
-            if ok(s + 3):
-                evacuate(s + 3)
             if ok(s - 2):
                 bias_relu(s - 2)
+            if ok(s + 3):
+                transposes(s + 3)
+            if ok(s - 2):
                 turn_back(s - 2)
+            if ok(s + 3):
+                evacuate(s + 3)
             if ok(s - 1):
                 blend_max(s - 1)
             if ok(s + 2):

@@ -240,7 +240,7 @@ def tile_complexnn_pa_t_kernel(tc, x, W1, b1, W2, b2, out):
                 in_=o_sb[:],
             )
 
-        for s in range(-4, NCH + 4):
+        for s in range(-4, NCH + 1):
             if ok(s + 4):
                 load(s + 4)
             if s == -4:
@@ -254,11 +254,12 @@ def tile_complexnn_pa_t_kernel(tc, x, W1, b1, W2, b2, out):
                 nc.vector.tensor_copy(out=b1f[:], in_=b1raw[:])
                 nc.vector.tensor_scalar_mul(out=b1s[:], in0=b1raw[:], scalar1=0.9)
                 w1_quant(3)
-            if ok(s - 2):
-                layer2(s - 2)
-            for j in range(PACK):
-                if ok(s):
-                    tanh(s, j)
+            if ok(s - 4):
+                store(s - 4)
+            if ok(s - 3):
+                bias_relu(s - 3)
+            if ok(s + 2):
+                evacuate(s + 2)
             for j in range(PACK):
                 if ok(s):
                     mix(s, j)
@@ -268,21 +269,29 @@ def tile_complexnn_pa_t_kernel(tc, x, W1, b1, W2, b2, out):
                     layer1(s + 1, j)
             if s == 0:
                 w2_prep()
-            if ok(s - 3):
-                store(s - 3)
             if ok(s):
                 affine(s, 2)
+            for j in range(PACK):
+                if ok(s + 1):
+                    tanh(s + 1, j)
             if ok(s - 2):
-                bias_relu(s - 2)
+                layer2(s - 2)
+            if ok(s - 3):
+                turn_back(s - 3)
             if ok(s + 3):
                 transposes(s + 3)
-            if ok(s - 2):
-                turn_back(s - 2)
-            if ok(s + 3):
-                evacuate(s + 3)
             if ok(s - 1):
                 blend_max(s - 1)
             if ok(s + 2):
                 quant_x(s + 2)
             if ok(s - 1):
                 quant_h(s - 1)
+
+        store(NCH - 3)
+        bias_relu(NCH - 2)
+        turn_back(NCH - 2)
+        store(NCH - 2)
+        layer2(NCH - 1)
+        bias_relu(NCH - 1)
+        turn_back(NCH - 1)
+        store(NCH - 1)

@@ -165,7 +165,7 @@ def tile_complexnn_pa_t_kernel(tc, x, W1, b1, W2, b2, out):
             )
 
         def affine(c, j):
-            if j != 2:
+            if j != 3:
                 nc.gpsimd.tensor_scalar(
                     out=live["y", c][:, :, j, 0:4],
                     in0=live["u", c][:, j, :].rearrange("p (c i) -> p c i", i=4),
@@ -263,14 +263,14 @@ def tile_complexnn_pa_t_kernel(tc, x, W1, b1, W2, b2, out):
             for j in range(PACK):
                 if ok(s):
                     mix(s, j)
-                    if j != 2:
+                    if j != 3:
                         affine(s, j)
                 if ok(s + 1):
                     layer1(s + 1, j)
             if s == 0:
                 w2_prep()
             if ok(s):
-                affine(s, 2)
+                affine(s, 3)
             for j in range(PACK):
                 if ok(s + 1):
                     tanh(s + 1, j)

@@ -94,7 +94,7 @@ def tile_complexnn_pa_t_kernel(tc, x, W1, b1, W2, b2, out):
             x_sb = xin.tile([P, R, D], BF16, name="x_sb")
             nc.sync.dma_start(
                 out=x_sb[:],
-                in_=x[c * CH : (c + 1) * CH, :].rearrange("(r p) k -> p r k", p=P),
+                in_=x[c * CH : (c + 1) * CH, :].rearrange("(p r) k -> p r k", r=R),
             )
             live["x", c] = x_sb
 
@@ -143,12 +143,12 @@ def tile_complexnn_pa_t_kernel(tc, x, W1, b1, W2, b2, out):
 
         def tanh(c, j):
             if j == 0:
-                live["t", c] = act.tile([P, CH // 4, PACK, 4], F32, name="t")
+                live["t", c] = act.tile([P, PACK, CH], F32, name="t")
                 live["u", c] = act.tile([P, PACK, CH], F32, name="u_t")
-                live["y", c] = act.tile([P, CH // 4, PACK, 8], F32, name="y")
+                live["y", c] = act.tile([P, PACK, CH], F32, name="y")
             nc.scalar.activation(
-                out=live["t", c][:, :, j, :],
-                in_=live["a", c, j][:].rearrange("p (c i) -> p c i", i=4),
+                out=live["t", c][:, j, :],
+                in_=live["a", c, j][:],
                 func=ACT.Tanh,
                 bias=b1f[:, j : j + 1],
                 scale=1.0,
@@ -156,10 +156,10 @@ def tile_complexnn_pa_t_kernel(tc, x, W1, b1, W2, b2, out):
 
         def mix(c, j):
             nc.vector.scalar_tensor_tensor(
-                out=live["u", c][:, j, :].rearrange("p (c i) -> p c i", i=4),
-                in0=live["t", c][:, :, j, :],
+                out=live["u", c][:, j, :],
+                in0=live["t", c][:, j, :],
                 scalar=1.0 / 9.0,
-                in1=live["a", c, j][:].rearrange("p (c i) -> p c i", i=4),
+                in1=live["a", c, j][:],
                 op0=ALU.mult,
                 op1=ALU.add,
             )
@@ -167,31 +167,29 @@ def tile_complexnn_pa_t_kernel(tc, x, W1, b1, W2, b2, out):
         def affine(c, j):
             if j != 3:
                 nc.gpsimd.tensor_scalar(
-                    out=live["y", c][:, :, j, 0:4],
-                    in0=live["u", c][:, j, :].rearrange("p (c i) -> p c i", i=4),
-                    scalar1=0.9,
+                    out=live["y", c][:, j, :],
+                    in0=live["u", c][:, j, :],
+                    scalar1=1.8,
                     scalar2=b1s[:, j : j + 1],
                     op0=ALU.mult,
                     op1=ALU.add,
                 )
             else:
                 nc.scalar.activation(
-                    out=live["y", c][:, :, j, 0:4],
-                    in_=live["u", c][:, j, :].rearrange("p (c i) -> p c i", i=4),
+                    out=live["y", c][:, j, :],
+                    in_=live["u", c][:, j, :],
                     func=ACT.Identity,
                     bias=b1s[:, j : j + 1],
-                    scale=0.9,
+                    scale=1.8,
                 )
 
         def blend_max(c):
-            hg = hgp.tile([P, 4, CH // 4, PACK], BF16, align_bytes=64, name="hg")
-            nc.vector.scalar_tensor_tensor(
-                out=hg[:].rearrange("p i c j -> p (c j) i"),
-                in0=live["t", c][:].rearrange("p c j i -> p (c j) i"),
-                scalar=0.5,
-                in1=live["y", c][:, :, :, 0:4].rearrange("p c j i -> p (c j) i"),
-                op0=ALU.mult,
-                op1=ALU.max,
+            hg = hgp.tile([P, CH, PACK], BF16, align_bytes=64, name="hg")
+            nc.vector.tensor_tensor(
+                out=hg[:].rearrange("p (c i) j -> p c j i", i=2),
+                in0=live["t", c][:].rearrange("p j (c i) -> p c j i", i=2),
+                in1=live["y", c][:].rearrange("p j (c i) -> p c j i", i=2),
+                op=ALU.max,
             )
             live["hg", c] = hg
 
@@ -201,7 +199,7 @@ def tile_complexnn_pa_t_kernel(tc, x, W1, b1, W2, b2, out):
             nc.vector.quantize_mx(
                 out=hq[:].bitcast(FP8X4),
                 scales=hs[:],
-                in_=live["hg", c][:].rearrange("p i c j -> p (i c j)"),
+                in_=live["hg", c][:].rearrange("p n j -> p (n j)"),
             )
             live["hq", c] = hq
             live["hs", c] = hs
@@ -222,7 +220,7 @@ def tile_complexnn_pa_t_kernel(tc, x, W1, b1, W2, b2, out):
         def bias_relu(c):
             o_t = outp.tile([P, CH], F32, name="o_t")
             nc.scalar.activation(
-                out=o_t[:], in_=live["o_ps", c][:], func=ACT.Relu, bias=b2f[:, 0:1], scale=1.0
+                out=o_t[:], in_=live["o_ps", c][:], func=ACT.Relu, bias=b2f[:, 0:1], scale=0.5
             )
             live["o_t", c] = o_t
 
@@ -252,7 +250,7 @@ def tile_complexnn_pa_t_kernel(tc, x, W1, b1, W2, b2, out):
                 w1_group(3)
                 w1_quant(2)
                 nc.vector.tensor_copy(out=b1f[:], in_=b1raw[:])
-                nc.vector.tensor_scalar_mul(out=b1s[:], in0=b1raw[:], scalar1=0.9)
+                nc.vector.tensor_scalar_mul(out=b1s[:], in0=b1raw[:], scalar1=1.8)
                 w1_quant(3)
             if ok(s - 4):
                 store(s - 4)

@@ -19,6 +19,7 @@ PACK = 4
 CH = 512
 R = CH // P
 NCH = B // CH
+GP_COLS = (512, 512, 256, 0)
 
 
 def tile_complexnn_pa_t_kernel(tc, x, W1, b1, W2, b2, out):
@@ -164,20 +165,24 @@ def tile_complexnn_pa_t_kernel(tc, x, W1, b1, W2, b2, out):
                 op1=ALU.add,
             )
 
-        def affine(c, j):
-            if j != 3:
+        def affine_gpsimd(c, j):
+            n = GP_COLS[j]
+            if n > 0:
                 nc.gpsimd.tensor_scalar(
-                    out=live["y", c][:, j, :],
-                    in0=live["u", c][:, j, :],
+                    out=live["y", c][:, j, :n],
+                    in0=live["u", c][:, j, :n],
                     scalar1=1.8,
                     scalar2=b1s[:, j : j + 1],
                     op0=ALU.mult,
                     op1=ALU.add,
                 )
-            else:
+
+        def affine_scalar(c, j):
+            n = GP_COLS[j]
+            if n < CH:
                 nc.scalar.activation(
-                    out=live["y", c][:, j, :],
-                    in_=live["u", c][:, j, :],
+                    out=live["y", c][:, j, n:],
+                    in_=live["u", c][:, j, n:],
                     func=ACT.Identity,
                     bias=b1s[:, j : j + 1],
                     scale=1.8,
@@ -261,14 +266,14 @@ def tile_complexnn_pa_t_kernel(tc, x, W1, b1, W2, b2, out):
             for j in range(PACK):
                 if ok(s):
                     mix(s, j)
-                    if j != 3:
-                        affine(s, j)
+                    affine_gpsimd(s, j)
                 if ok(s + 1):
                     layer1(s + 1, j)
             if s == 0:
                 w2_prep()
             if ok(s):
-                affine(s, 3)
+                for j in range(PACK):
+                    affine_scalar(s, j)
             for j in range(PACK):
                 if ok(s + 1):
                     tanh(s + 1, j)

@@ -19,7 +19,7 @@ PACK = 4
 CH = 512
 R = CH // P
 NCH = B // CH
-GP_COLS = (512, 512, 256, 0)
+GP_COLS = (512, 512, 384, 0)
 
 
 def tile_complexnn_pa_t_kernel(tc, x, W1, b1, W2, b2, out):
@@ -45,11 +45,6 @@ def tile_complexnn_pa_t_kernel(tc, x, W1, b1, W2, b2, out):
             return 0 <= c < NCH
 
         w1raw = const.tile([P, PACK, H], BF16)
-        for u in range(2):
-            nc.sync.dma_start(
-                out=w1raw[:, 2 * u : 2 * u + 2, :],
-                in_=W1[256 * u : 256 * (u + 1), :].rearrange("(p e) c -> p e c", e=2),
-            )
         b1raw = const.tile([P, PACK], BF16)
         nc.scalar.dma_start(out=b1raw[:], in_=b1.rearrange("(p j) -> p j", j=PACK))
         w2raw = const.tile([P, PACK, F], BF16)
@@ -65,12 +60,18 @@ def tile_complexnn_pa_t_kernel(tc, x, W1, b1, W2, b2, out):
         w2g = const.tile([P, F, PACK], BF16, align_bytes=64)
         w2q = const.tile([P, F], U32, align_bytes=64)
         w2s = const.tile([P, F], U8, align_bytes=64)
-        b1f = const.tile([P, PACK], F32)
         b1s = const.tile([P, PACK], F32)
         b2f = const.tile([P, 1], F32)
 
-        def w1_group(j):
-            nc.vector.tensor_copy(
+        def load_w1():
+            for u in range(2):
+                nc.sync.dma_start(
+                    out=w1raw[:, 2 * u : 2 * u + 2, :],
+                    in_=W1[256 * u : 256 * (u + 1), :].rearrange("(p e) c -> p e c", e=2),
+                )
+
+        def w1_group(copy, j):
+            copy(
                 out=w1g[:, j * P : (j + 1) * P, :],
                 in_=w1raw[:].rearrange("p t (m j) -> p j m t", j=PACK)[:, j],
             )
@@ -82,9 +83,7 @@ def tile_complexnn_pa_t_kernel(tc, x, W1, b1, W2, b2, out):
                 in_=w1g[:, j * P : (j + 1) * P, :].rearrange("p m t -> p (m t)"),
             )
 
-        def w2_prep():
-            nc.vector.tensor_copy(out=w2g[:], in_=w2raw[:].rearrange("p t f -> p f t"))
-            nc.vector.tensor_copy(out=b2f[:], in_=b2raw[:])
+        def w2_quant():
             nc.vector.quantize_mx(
                 out=w2q[:].bitcast(FP8X4),
                 scales=w2s[:],
@@ -93,10 +92,10 @@ def tile_complexnn_pa_t_kernel(tc, x, W1, b1, W2, b2, out):
 
         def load(c):
             x_sb = xin.tile([P, R, D], BF16, name="x_sb")
-            nc.sync.dma_start(
-                out=x_sb[:],
-                in_=x[c * CH : (c + 1) * CH, :].rearrange("(p r) k -> p r k", r=R),
-            )
+            rows = x[c * CH : (c + 1) * CH, :].rearrange("(p r) k -> p r k", r=R)
+            step = R // 2 if c == 0 else R
+            for r in range(0, R, step):
+                nc.sync.dma_start(out=x_sb[:, r : r + step, :], in_=rows[:, r : r + step, :])
             live["x", c] = x_sb
 
         def transposes(c):
@@ -151,7 +150,7 @@ def tile_complexnn_pa_t_kernel(tc, x, W1, b1, W2, b2, out):
                 out=live["t", c][:, j, :],
                 in_=live["a", c, j][:],
                 func=ACT.Tanh,
-                bias=b1f[:, j : j + 1],
+                bias=b1raw[:, j : j + 1],
                 scale=1.0,
             )
 
@@ -188,26 +187,25 @@ def tile_complexnn_pa_t_kernel(tc, x, W1, b1, W2, b2, out):
                     scale=1.8,
                 )
 
-        def blend_max(c):
-            hg = hgp.tile([P, CH, PACK], BF16, align_bytes=64, name="hg")
+        def blend_max(c, lo=0, hi=CH):
+            if lo == 0:
+                live["hg", c] = hgp.tile([P, CH, PACK], BF16, align_bytes=64, name="hg")
             nc.vector.tensor_tensor(
-                out=hg[:].rearrange("p (c i) j -> p c j i", i=2),
-                in0=live["t", c][:].rearrange("p j (c i) -> p c j i", i=2),
-                in1=live["y", c][:].rearrange("p j (c i) -> p c j i", i=2),
+                out=live["hg", c][:, lo:hi, :].rearrange("p (c i) j -> p c j i", i=2),
+                in0=live["t", c][:, :, lo:hi].rearrange("p j (c i) -> p c j i", i=2),
+                in1=live["y", c][:, :, lo:hi].rearrange("p j (c i) -> p c j i", i=2),
                 op=ALU.max,
             )
-            live["hg", c] = hg
 
-        def quant_h(c):
-            hq = hqp.tile([P, CH], U32, align_bytes=64, name="hq")
-            hs = hqp.tile([P, CH], U8, align_bytes=64, name="hs")
+        def quant_h(c, lo=0, hi=CH):
+            if lo == 0:
+                live["hq", c] = hqp.tile([P, CH], U32, align_bytes=64, name="hq")
+                live["hs", c] = hqp.tile([P, CH], U8, align_bytes=64, name="hs")
             nc.vector.quantize_mx(
-                out=hq[:].bitcast(FP8X4),
-                scales=hs[:],
-                in_=live["hg", c][:].rearrange("p n j -> p (n j)"),
+                out=live["hq", c][:, lo:hi].bitcast(FP8X4),
+                scales=live["hs", c][:, lo:hi],
+                in_=live["hg", c][:, lo:hi, :].rearrange("p n j -> p (n j)"),
             )
-            live["hq", c] = hq
-            live["hs", c] = hs
 
         def layer2(c):
             o_ps = ps_o.tile([P, CH], F32, name="o_ps")
@@ -225,7 +223,7 @@ def tile_complexnn_pa_t_kernel(tc, x, W1, b1, W2, b2, out):
         def bias_relu(c):
             o_t = outp.tile([P, CH], F32, name="o_t")
             nc.scalar.activation(
-                out=o_t[:], in_=live["o_ps", c][:], func=ACT.Relu, bias=b2f[:, 0:1], scale=0.5
+                out=o_t[:], in_=live["o_ps", c][:], func=ACT.Relu, bias=b2raw[:, 0:1], scale=0.5
             )
             live["o_t", c] = o_t
 
@@ -243,26 +241,36 @@ def tile_complexnn_pa_t_kernel(tc, x, W1, b1, W2, b2, out):
                 in_=o_sb[:],
             )
 
-        for s in range(-4, NCH + 1):
+        for s in range(-4, NCH):
             if ok(s + 4):
                 load(s + 4)
             if s == -4:
-                w1_group(0)
-                w1_group(1)
+                load_w1()
+                w1_group(nc.vector.tensor_copy, 0)
+                w1_group(nc.vector.tensor_copy, 1)
                 w1_quant(0)
-                w1_group(2)
                 w1_quant(1)
-                w1_group(3)
-                w1_quant(2)
-                nc.vector.tensor_copy(out=b1f[:], in_=b1raw[:])
-                nc.vector.tensor_scalar_mul(out=b1s[:], in0=b1raw[:], scalar1=1.8)
-                w1_quant(3)
+                nc.gpsimd.tensor_scalar(
+                    out=w2g[:],
+                    in0=w2raw[:].rearrange("p t f -> p f t"),
+                    scalar1=1.0,
+                    scalar2=0.0,
+                    op0=ALU.mult,
+                    op1=ALU.add,
+                )
+                nc.gpsimd.tensor_copy(out=b2f[:], in_=b2raw[:])
+                nc.gpsimd.tensor_scalar(
+                    out=b1s[:], in0=b1raw[:], scalar1=1.8, scalar2=0.0, op0=ALU.mult, op1=ALU.add
+                )
             if ok(s - 4):
                 store(s - 4)
             if ok(s - 3):
                 bias_relu(s - 3)
             if ok(s + 2):
                 evacuate(s + 2)
+            if s == -2:
+                w1_group(nc.scalar.copy, 2)
+                w1_group(nc.scalar.copy, 3)
             for j in range(PACK):
                 if ok(s):
                     mix(s, j)
@@ -270,7 +278,7 @@ def tile_complexnn_pa_t_kernel(tc, x, W1, b1, W2, b2, out):
                 if ok(s + 1):
                     layer1(s + 1, j)
             if s == 0:
-                w2_prep()
+                w2_quant()
             if ok(s):
                 for j in range(PACK):
                     affine_scalar(s, j)
@@ -287,14 +295,92 @@ def tile_complexnn_pa_t_kernel(tc, x, W1, b1, W2, b2, out):
                 blend_max(s - 1)
             if ok(s + 2):
                 quant_x(s + 2)
-            if ok(s - 1):
+            if s == -2:
+                w1_quant(2)
+                w1_quant(3)
+            if ok(s - 1) and s < NCH - 1:
                 quant_h(s - 1)
 
+        half = CH // 2
+
+        def layer2_half(h):
+            o_ps = ps_a.tile([P, CH], F32, name="a")
+            nc.tensor.matmul_mx(
+                out=o_ps[:, :half],
+                lhsT=w2q[:].bitcast(FP8X4),
+                lhsT_scale=w2s[:],
+                rhs=live["hq", NCH - 1][:, h * half : (h + 1) * half].bitcast(FP8X4),
+                rhs_scale=live["hs", NCH - 1][:, h * half : (h + 1) * half],
+                start=True,
+                stop=True,
+            )
+            live["o_ps", NCH - 1, h] = o_ps
+
+        def bias_half(h):
+            o_t = outp.tile([P, CH], F32, name="o_t")
+            if h == 0:
+                nc.scalar.activation(
+                    out=o_t[:, :half],
+                    in_=live["o_ps", NCH - 1, h][:, :half],
+                    func=ACT.Identity,
+                    bias=b2raw[:, 0:1],
+                    scale=0.5,
+                )
+            else:
+                nc.vector.tensor_scalar(
+                    out=o_t[:, :half],
+                    in0=live["o_ps", NCH - 1, h][:, :half],
+                    scalar1=0.5,
+                    scalar2=b2f[:, 0:1],
+                    op0=ALU.mult,
+                    op1=ALU.add,
+                )
+            live["o_t", NCH - 1, h] = o_t
+
+        def turn_back_half(h):
+            ot = ps_a.tile([P, CH], F32, name="a")
+            for r in range(R // 2):
+                nc.tensor.transpose(
+                    ot[:, r * F : (r + 1) * F],
+                    live["o_t", NCH - 1, h][:, r * P : (r + 1) * P],
+                    ident[:],
+                )
+            live["ot", NCH - 1, h] = ot
+
+        def store_half(h):
+            o_sb = outp.tile([P, R, F], F32, name="o_sb")
+            flat = o_sb[:].rearrange("p r f -> p (r f)")[:, : R // 2 * F]
+            if h == 0:
+                nc.scalar.activation(out=flat, in_=live["ot", NCH - 1, h][:, :half], func=ACT.Relu)
+            else:
+                nc.vector.tensor_scalar_max(
+                    out=flat, in0=live["ot", NCH - 1, h][:, :half], scalar1=0.0
+                )
+            nc.sync.dma_start(
+                out=out[(NCH - 1) * CH :, :].rearrange("(p r) f -> p r f", r=R)[
+                    :, h * (R // 2) : (h + 1) * (R // 2), :
+                ],
+                in_=o_sb[:, : R // 2, :],
+            )
+
+        store(NCH - 4)
+        bias_relu(NCH - 3)
+        turn_back(NCH - 3)
+        blend_max(NCH - 1, 0, half)
+        quant_h(NCH - 2)
+        blend_max(NCH - 1, half, CH)
+        layer2(NCH - 2)
+        quant_h(NCH - 1, 0, half)
+        quant_h(NCH - 1, half, CH)
         store(NCH - 3)
         bias_relu(NCH - 2)
+        layer2_half(0)
+        layer2_half(1)
+        bias_half(0)
+        bias_half(1)
         turn_back(NCH - 2)
+        turn_back_half(0)
+        turn_back_half(1)
+        store_half(0)
+        store_half(1)
         store(NCH - 2)
-        layer2(NCH - 1)
-        bias_relu(NCH - 1)
-        turn_back(NCH - 1)
-        store(NCH - 1)

@@ -17,9 +17,10 @@ FLOPS = 2 * B * D * H + 2 * B * H * F
 P = 128
 PACK = 4
 CH = 512
-R = CH // P
-NCH = B // CH
-GP_COLS = (512, 512, 384, 0)
+WIDTHS = (CH // 2,) + (CH,) * (B // CH - 1) + (CH // 4, CH // 4)
+NCH = len(WIDTHS)
+ROW0 = tuple(sum(WIDTHS[:c]) for c in range(NCH))
+GP_SHARE = (4, 3, 3, 0)
 
 
 def tile_complexnn_pa_t_kernel(tc, x, W1, b1, W2, b2, out):
@@ -91,18 +92,20 @@ def tile_complexnn_pa_t_kernel(tc, x, W1, b1, W2, b2, out):
             )
 
         def load(c):
-            x_sb = xin.tile([P, R, D], BF16, name="x_sb")
-            rows = x[c * CH : (c + 1) * CH, :].rearrange("(p r) k -> p r k", r=R)
-            step = R // 2 if c == 0 else R
-            for r in range(0, R, step):
-                nc.sync.dma_start(out=x_sb[:, r : r + step, :], in_=rows[:, r : r + step, :])
+            w = WIDTHS[c]
+            x_sb = xin.tile([P, w // P, D], BF16, name="x_sb")
+            nc.sync.dma_start(
+                out=x_sb[:],
+                in_=x[ROW0[c] : ROW0[c] + w, :].rearrange("(p r) k -> p r k", r=w // P),
+            )
             live["x", c] = x_sb
 
         def transposes(c):
             xw = live["x", c][:].bitcast(F32)
-            for i in range(2):
+            tiles = WIDTHS[c] // P
+            for i in range((tiles + 1) // 2):
                 xt = ps_x.tile([P, 2, 2, P], F32, name="xt")
-                for rr in range(2):
+                for rr in range(min(2, tiles - 2 * i)):
                     for u in range(2):
                         nc.tensor.transpose(
                             xt[:, rr, u, :], xw[:, 2 * i + rr, u * P : (u + 1) * P], ident[:]
@@ -110,28 +113,31 @@ def tile_complexnn_pa_t_kernel(tc, x, W1, b1, W2, b2, out):
                 live["xt", c, i] = xt
 
         def evacuate(c):
-            xg = xgp.tile([P, CH * PACK], BF16, align_bytes=64, name="xg")
+            xg = xgp.tile([P, WIDTHS[c] * PACK], BF16, align_bytes=64, name="xg")
             xg32 = xg[:].bitcast(F32)
-            for i in range(2):
+            tiles = WIDTHS[c] // P
+            for i in range((tiles + 1) // 2):
+                n = min(2, tiles - 2 * i)
                 nc.scalar.copy(
-                    out=xg32[:, 512 * i : 512 * (i + 1)].rearrange(
-                        "p (r b u) -> p r b u", r=2, u=2
+                    out=xg32[:, 512 * i : 512 * i + 256 * n].rearrange(
+                        "p (r b u) -> p r b u", r=n, u=2
                     ),
-                    in_=live["xt", c, i][:].rearrange("p r u b -> p r b u"),
+                    in_=live["xt", c, i][:, :n].rearrange("p r u b -> p r b u"),
                 )
             live["xg", c] = xg
 
         def quant_x(c):
-            xq = xqp.tile([P, CH], U32, align_bytes=64, name="xq")
-            xs = xqp.tile([P, CH], U8, align_bytes=64, name="xs")
+            xq = xqp.tile([P, WIDTHS[c]], U32, align_bytes=64, name="xq")
+            xs = xqp.tile([P, WIDTHS[c]], U8, align_bytes=64, name="xs")
             nc.vector.quantize_mx(out=xq[:].bitcast(FP8X4), scales=xs[:], in_=live["xg", c][:])
             live["xq", c] = xq
             live["xs", c] = xs
 
         def layer1(c, j):
-            a = ps_a.tile([P, CH], F32, name="a")
+            bank = ps_a.tile([P, CH], F32, name="a")
+            a = bank[:, : WIDTHS[c]]
             nc.tensor.matmul_mx(
-                out=a[:],
+                out=a,
                 lhsT=w1q[:, j * P : (j + 1) * P].bitcast(FP8X4),
                 lhsT_scale=w1s[:, j * P : (j + 1) * P],
                 rhs=live["xq", c][:].bitcast(FP8X4),
@@ -143,12 +149,12 @@ def tile_complexnn_pa_t_kernel(tc, x, W1, b1, W2, b2, out):
 
         def tanh(c, j):
             if j == 0:
-                live["t", c] = act.tile([P, PACK, CH], F32, name="t")
-                live["u", c] = act.tile([P, PACK, CH], F32, name="u_t")
-                live["y", c] = act.tile([P, PACK, CH], F32, name="y")
+                live["t", c] = act.tile([P, PACK, WIDTHS[c]], F32, name="t")
+                live["u", c] = act.tile([P, PACK, WIDTHS[c]], F32, name="u_t")
+                live["y", c] = act.tile([P, PACK, WIDTHS[c]], F32, name="y")
             nc.scalar.activation(
                 out=live["t", c][:, j, :],
-                in_=live["a", c, j][:],
+                in_=live["a", c, j],
                 func=ACT.Tanh,
                 bias=b1raw[:, j : j + 1],
                 scale=1.0,
@@ -159,13 +165,13 @@ def tile_complexnn_pa_t_kernel(tc, x, W1, b1, W2, b2, out):
                 out=live["u", c][:, j, :],
                 in0=live["t", c][:, j, :],
                 scalar=1.0 / 9.0,
-                in1=live["a", c, j][:],
+                in1=live["a", c, j],
                 op0=ALU.mult,
                 op1=ALU.add,
             )
 
         def affine_gpsimd(c, j):
-            n = GP_COLS[j]
+            n = WIDTHS[c] * GP_SHARE[j] // 4
             if n > 0:
                 nc.gpsimd.tensor_scalar(
                     out=live["y", c][:, j, :n],
@@ -177,8 +183,8 @@ def tile_complexnn_pa_t_kernel(tc, x, W1, b1, W2, b2, out):
                 )
 
         def affine_scalar(c, j):
-            n = GP_COLS[j]
-            if n < CH:
+            n = WIDTHS[c] * GP_SHARE[j] // 4
+            if n < WIDTHS[c]:
                 nc.scalar.activation(
                     out=live["y", c][:, j, n:],
                     in_=live["u", c][:, j, n:],
@@ -187,30 +193,35 @@ def tile_complexnn_pa_t_kernel(tc, x, W1, b1, W2, b2, out):
                     scale=1.8,
                 )
 
-        def blend_max(c, lo=0, hi=CH):
-            if lo == 0:
-                live["hg", c] = hgp.tile([P, CH, PACK], BF16, align_bytes=64, name="hg")
+        def blend_max(c):
+            hg = hgp.tile([P, WIDTHS[c], PACK], BF16, align_bytes=64, name="hg")
             nc.vector.tensor_tensor(
-                out=live["hg", c][:, lo:hi, :].rearrange("p (c i) j -> p c j i", i=2),
-                in0=live["t", c][:, :, lo:hi].rearrange("p j (c i) -> p c j i", i=2),
-                in1=live["y", c][:, :, lo:hi].rearrange("p j (c i) -> p c j i", i=2),
+                out=hg[:].rearrange("p (c i) j -> p c j i", i=2),
+                in0=live["t", c][:].rearrange("p j (c i) -> p c j i", i=2),
+                in1=live["y", c][:].rearrange("p j (c i) -> p c j i", i=2),
                 op=ALU.max,
             )
+            live["hg", c] = hg
 
-        def quant_h(c, lo=0, hi=CH):
-            if lo == 0:
-                live["hq", c] = hqp.tile([P, CH], U32, align_bytes=64, name="hq")
-                live["hs", c] = hqp.tile([P, CH], U8, align_bytes=64, name="hs")
+        def quant_h(c):
+            hq = hqp.tile([P, WIDTHS[c]], U32, align_bytes=64, name="hq")
+            hs = hqp.tile([P, WIDTHS[c]], U8, align_bytes=64, name="hs")
             nc.vector.quantize_mx(
-                out=live["hq", c][:, lo:hi].bitcast(FP8X4),
-                scales=live["hs", c][:, lo:hi],
-                in_=live["hg", c][:, lo:hi, :].rearrange("p n j -> p (n j)"),
+                out=hq[:].bitcast(FP8X4),
+                scales=hs[:],
+                in_=live["hg", c][:].rearrange("p n j -> p (n j)"),
             )
+            live["hq", c] = hq
+            live["hs", c] = hs
 
         def layer2(c):
-            o_ps = ps_o.tile([P, CH], F32, name="o_ps")
+            if c < NCH - 2:
+                bank = ps_o.tile([P, CH], F32, name="o_ps")
+            else:
+                bank = ps_a.tile([P, CH], F32, name="a")
+            o_ps = bank[:, : WIDTHS[c]]
             nc.tensor.matmul_mx(
-                out=o_ps[:],
+                out=o_ps,
                 lhsT=w2q[:].bitcast(FP8X4),
                 lhsT_scale=w2s[:],
                 rhs=live["hq", c][:].bitcast(FP8X4),
@@ -221,23 +232,43 @@ def tile_complexnn_pa_t_kernel(tc, x, W1, b1, W2, b2, out):
             live["o_ps", c] = o_ps
 
         def bias_relu(c):
-            o_t = outp.tile([P, CH], F32, name="o_t")
-            nc.scalar.activation(
-                out=o_t[:], in_=live["o_ps", c][:], func=ACT.Relu, bias=b2raw[:, 0:1], scale=0.5
-            )
+            o_t = outp.tile([P, WIDTHS[c]], F32, name="o_t")
+            if c < NCH - 1:
+                nc.scalar.activation(
+                    out=o_t[:], in_=live["o_ps", c], func=ACT.Relu, bias=b2raw[:, 0:1], scale=0.5
+                )
+            else:
+                nc.vector.tensor_scalar(
+                    out=o_t[:],
+                    in0=live["o_ps", c],
+                    scalar1=0.5,
+                    scalar2=b2f[:, 0:1],
+                    op0=ALU.mult,
+                    op1=ALU.add,
+                )
             live["o_t", c] = o_t
 
         def turn_back(c):
-            ot = ps_t.tile([P, R, F], F32, name="ot")
-            for r in range(R):
-                nc.tensor.transpose(ot[:, r, :], live["o_t", c][:, r * P : (r + 1) * P], ident[:])
+            if c < NCH - 2:
+                bank = ps_t.tile([P, CH], F32, name="ot")
+            else:
+                bank = ps_a.tile([P, CH], F32, name="a")
+            ot = bank[:, : WIDTHS[c]]
+            for r in range(WIDTHS[c] // P):
+                cols = slice(r * P, (r + 1) * P)
+                nc.tensor.transpose(ot[:, cols], live["o_t", c][:, cols], ident[:])
             live["ot", c] = ot
 
         def store(c):
-            o_sb = outp.tile([P, R, F], F32, name="o_sb")
-            nc.scalar.copy(out=o_sb[:], in_=live["ot", c][:])
+            o_sb = outp.tile([P, WIDTHS[c]], F32, name="o_sb")
+            if c < NCH - 1:
+                nc.scalar.copy(out=o_sb[:], in_=live["ot", c])
+            else:
+                nc.vector.tensor_scalar_max(out=o_sb[:], in0=live["ot", c], scalar1=0.0)
             nc.sync.dma_start(
-                out=out[c * CH : (c + 1) * CH, :].rearrange("(p r) f -> p r f", r=R),
+                out=out[ROW0[c] : ROW0[c] + WIDTHS[c], :].rearrange(
+                    "(p r) f -> p (r f)", r=WIDTHS[c] // P
+                ),
                 in_=o_sb[:],
             )
 
@@ -301,86 +332,18 @@ def tile_complexnn_pa_t_kernel(tc, x, W1, b1, W2, b2, out):
             if ok(s - 1) and s < NCH - 1:
                 quant_h(s - 1)
 
-        half = CH // 2
-
-        def layer2_half(h):
-            o_ps = ps_a.tile([P, CH], F32, name="a")
-            nc.tensor.matmul_mx(
-                out=o_ps[:, :half],
-                lhsT=w2q[:].bitcast(FP8X4),
-                lhsT_scale=w2s[:],
-                rhs=live["hq", NCH - 1][:, h * half : (h + 1) * half].bitcast(FP8X4),
-                rhs_scale=live["hs", NCH - 1][:, h * half : (h + 1) * half],
-                start=True,
-                stop=True,
-            )
-            live["o_ps", NCH - 1, h] = o_ps
-
-        def bias_half(h):
-            o_t = outp.tile([P, CH], F32, name="o_t")
-            if h == 0:
-                nc.scalar.activation(
-                    out=o_t[:, :half],
-                    in_=live["o_ps", NCH - 1, h][:, :half],
-                    func=ACT.Identity,
-                    bias=b2raw[:, 0:1],
-                    scale=0.5,
-                )
-            else:
-                nc.vector.tensor_scalar(
-                    out=o_t[:, :half],
-                    in0=live["o_ps", NCH - 1, h][:, :half],
-                    scalar1=0.5,
-                    scalar2=b2f[:, 0:1],
-                    op0=ALU.mult,
-                    op1=ALU.add,
-                )
-            live["o_t", NCH - 1, h] = o_t
-
-        def turn_back_half(h):
-            ot = ps_a.tile([P, CH], F32, name="a")
-            for r in range(R // 2):
-                nc.tensor.transpose(
-                    ot[:, r * F : (r + 1) * F],
-                    live["o_t", NCH - 1, h][:, r * P : (r + 1) * P],
-                    ident[:],
-                )
-            live["ot", NCH - 1, h] = ot
-
-        def store_half(h):
-            o_sb = outp.tile([P, R, F], F32, name="o_sb")
-            flat = o_sb[:].rearrange("p r f -> p (r f)")[:, : R // 2 * F]
-            if h == 0:
-                nc.scalar.activation(out=flat, in_=live["ot", NCH - 1, h][:, :half], func=ACT.Relu)
-            else:
-                nc.vector.tensor_scalar_max(
-                    out=flat, in0=live["ot", NCH - 1, h][:, :half], scalar1=0.0
-                )
-            nc.sync.dma_start(
-                out=out[(NCH - 1) * CH :, :].rearrange("(p r) f -> p r f", r=R)[
-                    :, h * (R // 2) : (h + 1) * (R // 2), :
-                ],
-                in_=o_sb[:, : R // 2, :],
-            )
-
         store(NCH - 4)
         bias_relu(NCH - 3)
         turn_back(NCH - 3)
-        blend_max(NCH - 1, 0, half)
+        blend_max(NCH - 1)
         quant_h(NCH - 2)
-        blend_max(NCH - 1, half, CH)
+        quant_h(NCH - 1)
         layer2(NCH - 2)
-        quant_h(NCH - 1, 0, half)
-        quant_h(NCH - 1, half, CH)
-        store(NCH - 3)
+        layer2(NCH - 1)
         bias_relu(NCH - 2)
-        layer2_half(0)
-        layer2_half(1)
-        bias_half(0)
-        bias_half(1)
+        bias_relu(NCH - 1)
+        store(NCH - 3)
         turn_back(NCH - 2)
-        turn_back_half(0)
-        turn_back_half(1)
-        store_half(0)
-        store_half(1)
+        turn_back(NCH - 1)
         store(NCH - 2)
+        store(NCH - 1)

@@ -47,11 +47,8 @@ def tile_complexnn_pa_t_kernel(tc, x, W1, b1, W2, b2, out):
 
         w1raw = const.tile([P, PACK, H], BF16)
         b1raw = const.tile([P, PACK], BF16)
-        nc.scalar.dma_start(out=b1raw[:], in_=b1.rearrange("(p j) -> p j", j=PACK))
         w2raw = const.tile([P, PACK, F], BF16)
-        nc.scalar.dma_start(out=w2raw[:], in_=W2.rearrange("(p t) f -> p t f", t=PACK))
         b2raw = const.tile([P, 1], BF16)
-        nc.scalar.dma_start(out=b2raw[:], in_=b2.rearrange("(p o) -> p o", o=1))
         ident = const.tile([P, P], F32)
         make_identity(nc, ident[:])
 
@@ -63,6 +60,7 @@ def tile_complexnn_pa_t_kernel(tc, x, W1, b1, W2, b2, out):
         w2s = const.tile([P, F], U8, align_bytes=64)
         b1s = const.tile([P, PACK], F32)
         b2f = const.tile([P, 1], F32)
+        b2row = const.tile([P, F], F32)
 
         def load_w1():
             for u in range(2):
@@ -70,6 +68,11 @@ def tile_complexnn_pa_t_kernel(tc, x, W1, b1, W2, b2, out):
                     out=w1raw[:, 2 * u : 2 * u + 2, :],
                     in_=W1[256 * u : 256 * (u + 1), :].rearrange("(p e) c -> p e c", e=2),
                 )
+
+        def load_small():
+            nc.sync.dma_start(out=b1raw[:], in_=b1.rearrange("(p j) -> p j", j=PACK))
+            nc.sync.dma_start(out=w2raw[:], in_=W2.rearrange("(p t) f -> p t f", t=PACK))
+            nc.sync.dma_start(out=b2raw[:], in_=b2.rearrange("(p o) -> p o", o=1))
 
         def w1_group(copy, j):
             copy(
@@ -90,6 +93,16 @@ def tile_complexnn_pa_t_kernel(tc, x, W1, b1, W2, b2, out):
                 scales=w2s[:],
                 in_=w2g[:].rearrange("p f t -> p (f t)"),
             )
+
+        def b2_spread():
+            spread = ps_t.tile([P, CH], F32, name="ot")
+            nc.tensor.matmul(
+                spread[:, :F], b2f[:, 0:1].to_broadcast([P, P]), ident[:], start=True, stop=True
+            )
+            live["spread"] = spread
+
+        def b2_copy():
+            nc.scalar.copy(out=b2row[:], in_=live["spread"][:, :F])
 
         def load(c):
             w = WIDTHS[c]
@@ -115,10 +128,11 @@ def tile_complexnn_pa_t_kernel(tc, x, W1, b1, W2, b2, out):
         def evacuate(c):
             xg = xgp.tile([P, WIDTHS[c] * PACK], BF16, align_bytes=64, name="xg")
             xg32 = xg[:].bitcast(F32)
+            copy = nc.vector.tensor_copy if c == 1 else nc.scalar.copy
             tiles = WIDTHS[c] // P
             for i in range((tiles + 1) // 2):
                 n = min(2, tiles - 2 * i)
-                nc.scalar.copy(
+                copy(
                     out=xg32[:, 512 * i : 512 * i + 256 * n].rearrange(
                         "p (r b u) -> p r b u", r=n, u=2
                     ),
@@ -215,10 +229,7 @@ def tile_complexnn_pa_t_kernel(tc, x, W1, b1, W2, b2, out):
             live["hs", c] = hs
 
         def layer2(c):
-            if c < NCH - 2:
-                bank = ps_o.tile([P, CH], F32, name="o_ps")
-            else:
-                bank = ps_a.tile([P, CH], F32, name="a")
+            bank = ps_o.tile([P, CH], F32, name="o_ps")
             o_ps = bank[:, : WIDTHS[c]]
             nc.tensor.matmul_mx(
                 out=o_ps,
@@ -233,26 +244,13 @@ def tile_complexnn_pa_t_kernel(tc, x, W1, b1, W2, b2, out):
 
         def bias_relu(c):
             o_t = outp.tile([P, WIDTHS[c]], F32, name="o_t")
-            if c < NCH - 1:
-                nc.scalar.activation(
-                    out=o_t[:], in_=live["o_ps", c], func=ACT.Relu, bias=b2raw[:, 0:1], scale=0.5
-                )
-            else:
-                nc.vector.tensor_scalar(
-                    out=o_t[:],
-                    in0=live["o_ps", c],
-                    scalar1=0.5,
-                    scalar2=b2f[:, 0:1],
-                    op0=ALU.mult,
-                    op1=ALU.add,
-                )
+            nc.scalar.activation(
+                out=o_t[:], in_=live["o_ps", c], func=ACT.Relu, bias=b2raw[:, 0:1], scale=0.5
+            )
             live["o_t", c] = o_t
 
         def turn_back(c):
-            if c < NCH - 2:
-                bank = ps_t.tile([P, CH], F32, name="ot")
-            else:
-                bank = ps_a.tile([P, CH], F32, name="a")
+            bank = ps_t.tile([P, CH], F32, name="ot")
             ot = bank[:, : WIDTHS[c]]
             for r in range(WIDTHS[c] // P):
                 cols = slice(r * P, (r + 1) * P)
@@ -261,10 +259,7 @@ def tile_complexnn_pa_t_kernel(tc, x, W1, b1, W2, b2, out):
 
         def store(c):
             o_sb = outp.tile([P, WIDTHS[c]], F32, name="o_sb")
-            if c < NCH - 1:
-                nc.scalar.copy(out=o_sb[:], in_=live["ot", c])
-            else:
-                nc.vector.tensor_scalar_max(out=o_sb[:], in0=live["ot", c], scalar1=0.0)
+            nc.scalar.copy(out=o_sb[:], in_=live["ot", c])
             nc.sync.dma_start(
                 out=out[ROW0[c] : ROW0[c] + WIDTHS[c], :].rearrange(
                     "(p r) f -> p (r f)", r=WIDTHS[c] // P
@@ -272,15 +267,42 @@ def tile_complexnn_pa_t_kernel(tc, x, W1, b1, W2, b2, out):
                 in_=o_sb[:],
             )
 
+        def layer2_rows(c):
+            bank = ps_a.tile([P, CH], F32, name="a")
+            o_ps = bank[:, :F]
+            nc.tensor.matmul_mx(
+                out=o_ps,
+                lhsT=live["hq", c][:].bitcast(FP8X4),
+                lhsT_scale=live["hs", c][:],
+                rhs=w2q[:].bitcast(FP8X4),
+                rhs_scale=w2s[:],
+                start=True,
+                stop=True,
+            )
+            live["o_ps", c] = o_ps
+
+        def bias_rows(c):
+            o_t = outp.tile([P, F], F32, name="o_t")
+            nc.vector.scalar_tensor_tensor(
+                out=o_t[:],
+                in0=live["o_ps", c],
+                scalar=0.5,
+                in1=b2row[:],
+                op0=ALU.mult,
+                op1=ALU.add,
+            )
+            live["o_t", c] = o_t
+
+        def store_rows(c):
+            o_sb = outp.tile([P, F], F32, name="o_sb")
+            nc.vector.tensor_scalar_max(out=o_sb[:], in0=live["o_t", c][:], scalar1=0.0)
+            nc.sync.dma_start(out=out[ROW0[c] : ROW0[c] + P, :], in_=o_sb[:])
+
         for s in range(-4, NCH):
             if ok(s + 4):
                 load(s + 4)
-            if s == -4:
-                load_w1()
-                w1_group(nc.vector.tensor_copy, 0)
-                w1_group(nc.vector.tensor_copy, 1)
-                w1_quant(0)
-                w1_quant(1)
+            if s == -3:
+                load_small()
                 nc.gpsimd.tensor_scalar(
                     out=w2g[:],
                     in0=w2raw[:].rearrange("p t f -> p f t"),
@@ -293,6 +315,12 @@ def tile_complexnn_pa_t_kernel(tc, x, W1, b1, W2, b2, out):
                 nc.gpsimd.tensor_scalar(
                     out=b1s[:], in0=b1raw[:], scalar1=1.8, scalar2=0.0, op0=ALU.mult, op1=ALU.add
                 )
+            if s == -4:
+                load_w1()
+                w1_group(nc.vector.tensor_copy, 0)
+                w1_group(nc.vector.tensor_copy, 1)
+                w1_quant(0)
+                w1_quant(1)
             if ok(s - 4):
                 store(s - 4)
             if ok(s - 3):
@@ -322,6 +350,10 @@ def tile_complexnn_pa_t_kernel(tc, x, W1, b1, W2, b2, out):
                 turn_back(s - 3)
             if ok(s + 3):
                 transposes(s + 3)
+            if s == -1:
+                b2_spread()
+            if s == 2:
+                b2_copy()
             if ok(s - 1):
                 blend_max(s - 1)
             if ok(s + 2):
@@ -338,12 +370,10 @@ def tile_complexnn_pa_t_kernel(tc, x, W1, b1, W2, b2, out):
         blend_max(NCH - 1)
         quant_h(NCH - 2)
         quant_h(NCH - 1)
-        layer2(NCH - 2)
-        layer2(NCH - 1)
-        bias_relu(NCH - 2)
-        bias_relu(NCH - 1)
+        layer2_rows(NCH - 2)
+        layer2_rows(NCH - 1)
+        bias_rows(NCH - 2)
+        bias_rows(NCH - 1)
         store(NCH - 3)
-        turn_back(NCH - 2)
-        turn_back(NCH - 1)
-        store(NCH - 2)
-        store(NCH - 1)
+        store_rows(NCH - 2)
+        store_rows(NCH - 1)

@@ -210,9 +210,9 @@ def tile_complexnn_pa_t_kernel(tc, x, W1, b1, W2, b2, out):
         def blend_max(c):
             hg = hgp.tile([P, WIDTHS[c], PACK], BF16, align_bytes=64, name="hg")
             nc.vector.tensor_tensor(
-                out=hg[:].rearrange("p (c i) j -> p c j i", i=2),
-                in0=live["t", c][:].rearrange("p j (c i) -> p c j i", i=2),
-                in1=live["y", c][:].rearrange("p j (c i) -> p c j i", i=2),
+                out=hg[:].rearrange("p (c i) j -> p c j i", i=4),
+                in0=live["t", c][:].rearrange("p j (c i) -> p c j i", i=4),
+                in1=live["y", c][:].rearrange("p j (c i) -> p c j i", i=4),
                 op=ALU.max,
             )
             live["hg", c] = hg

@@ -17,7 +17,7 @@ FLOPS = 2 * B * D * H + 2 * B * H * F
 P = 128
 PACK = 4
 CH = 512
-WIDTHS = (CH // 2,) + (CH,) * (B // CH - 1) + (CH // 4, CH // 4)
+WIDTHS = (CH // 2, CH // 2) + (CH,) * (B // CH - 2) + (CH // 2, CH // 4, CH // 4)
 NCH = len(WIDTHS)
 ROW0 = tuple(sum(WIDTHS[:c]) for c in range(NCH))
 GP_SHARE = (4, 3, 3, 0)
@@ -229,7 +229,10 @@ def tile_complexnn_pa_t_kernel(tc, x, W1, b1, W2, b2, out):
             live["hs", c] = hs
 
         def layer2(c):
-            bank = ps_o.tile([P, CH], F32, name="o_ps")
+            if c < NCH - 3:
+                bank = ps_o.tile([P, CH], F32, name="o_ps")
+            else:
+                bank = ps_x.tile([P, CH], F32, name="xt")
             o_ps = bank[:, : WIDTHS[c]]
             nc.tensor.matmul_mx(
                 out=o_ps,
@@ -250,7 +253,10 @@ def tile_complexnn_pa_t_kernel(tc, x, W1, b1, W2, b2, out):
             live["o_t", c] = o_t
 
         def turn_back(c):
-            bank = ps_t.tile([P, CH], F32, name="ot")
+            if c < NCH - 3:
+                bank = ps_t.tile([P, CH], F32, name="ot")
+            else:
+                bank = ps_x.tile([P, CH], F32, name="xt")
             ot = bank[:, : WIDTHS[c]]
             for r in range(WIDTHS[c] // P):
                 cols = slice(r * P, (r + 1) * P)
@@ -298,7 +304,7 @@ def tile_complexnn_pa_t_kernel(tc, x, W1, b1, W2, b2, out):
             nc.vector.tensor_scalar_max(out=o_sb[:], in0=live["o_t", c][:], scalar1=0.0)
             nc.sync.dma_start(out=out[ROW0[c] : ROW0[c] + P, :], in_=o_sb[:])
 
-        for s in range(-4, NCH):
+        for s in range(-4, NCH - 1):
             if ok(s + 4):
                 load(s + 4)
             if s == -3:
@@ -361,19 +367,30 @@ def tile_complexnn_pa_t_kernel(tc, x, W1, b1, W2, b2, out):
             if s == -2:
                 w1_quant(2)
                 w1_quant(3)
-            if ok(s - 1) and s < NCH - 1:
+            if ok(s - 1):
                 quant_h(s - 1)
 
-        store(NCH - 4)
-        bias_relu(NCH - 3)
-        turn_back(NCH - 3)
-        blend_max(NCH - 1)
-        quant_h(NCH - 2)
-        quant_h(NCH - 1)
-        layer2_rows(NCH - 2)
-        layer2_rows(NCH - 1)
-        bias_rows(NCH - 2)
-        bias_rows(NCH - 1)
-        store(NCH - 3)
-        store_rows(NCH - 2)
-        store_rows(NCH - 1)
+        end = NCH - 1
+        store(end - 4)
+        bias_relu(end - 3)
+        for j in range(PACK):
+            mix(end, j)
+            affine_gpsimd(end, j)
+        layer2(end - 2)
+        turn_back(end - 3)
+        bias_relu(end - 2)
+        turn_back(end - 2)
+        for j in range(PACK):
+            affine_scalar(end, j)
+        store(end - 3)
+        store(end - 2)
+        blend_max(end - 1)
+        blend_max(end)
+        quant_h(end - 1)
+        quant_h(end)
+        layer2_rows(end - 1)
+        layer2_rows(end)
+        bias_rows(end - 1)
+        bias_rows(end)
+        store_rows(end - 1)
+        store_rows(end)

from contextlib import ExitStack

import concourse.mybir as mybir
from concourse.masks import make_identity

F32 = mybir.dt.float32
BF16 = mybir.dt.bfloat16
U32 = mybir.dt.uint32
U8 = mybir.dt.uint8
FP8X4 = mybir.dt.float8_e4m3fn_x4
ACT = mybir.ActivationFunctionType
ALU = mybir.AluOpType

B, D, H, F = 16384, 512, 512, 128
FLOPS = 2 * B * D * H + 2 * B * H * F

P = 128
PACK = 4
CH = 512
WIDTHS = (CH // 2, CH // 2) + (CH,) * (B // CH - 2) + (CH // 2, CH // 4, CH // 4)
NCH = len(WIDTHS)
ROW0 = tuple(sum(WIDTHS[:c]) for c in range(NCH))
GP_SHARE = (4, 3, 3, 0)


def tile_complexnn_pa_t_kernel(tc, x, W1, b1, W2, b2, out):
    nc = tc.nc
    with ExitStack() as ctx:
        const = ctx.enter_context(tc.tile_pool(name="const", bufs=1))
        xin = ctx.enter_context(tc.tile_pool(name="xin", bufs=5))
        xgp = ctx.enter_context(tc.tile_pool(name="xgp", bufs=2))
        xqp = ctx.enter_context(tc.tile_pool(name="xqp", bufs=2))
        act = ctx.enter_context(tc.tile_pool(name="act", bufs=3))
        hgp = ctx.enter_context(tc.tile_pool(name="hgp", bufs=2))
        hqp = ctx.enter_context(tc.tile_pool(name="hqp", bufs=2))
        outp = ctx.enter_context(tc.tile_pool(name="outp", bufs=4))
        ps_x = ctx.enter_context(tc.psum_pool(name="ps_x", bufs=2))
        ps_a = ctx.enter_context(tc.psum_pool(name="ps_a", bufs=4))
        ps_o = ctx.enter_context(tc.psum_pool(name="ps_o", bufs=1))
        ps_t = ctx.enter_context(tc.psum_pool(name="ps_t", bufs=1))
        ctx.enter_context(tc.manual_schedule())

        live = {}

        def ok(c):
            return 0 <= c < NCH

        w1raw = const.tile([P, PACK, H], BF16)
        b1raw = const.tile([P, PACK], BF16)
        w2raw = const.tile([P, PACK, F], BF16)
        b2raw = const.tile([P, 1], BF16)
        ident = const.tile([P, P], F32)
        make_identity(nc, ident[:])

        w1g = const.tile([P, H, PACK], BF16, align_bytes=64)
        w1q = const.tile([P, H], U32, align_bytes=64)
        w1s = const.tile([P, H], U8, align_bytes=64)
        w2g = const.tile([P, F, PACK], BF16, align_bytes=64)
        w2q = const.tile([P, F], U32, align_bytes=64)
        w2s = const.tile([P, F], U8, align_bytes=64)
        b1s = const.tile([P, PACK], F32)
        b2f = const.tile([P, 1], F32)
        b2row = const.tile([P, F], F32)

        def load_w1():
            for u in range(2):
                nc.sync.dma_start(
                    out=w1raw[:, 2 * u : 2 * u + 2, :],
                    in_=W1[256 * u : 256 * (u + 1), :].rearrange("(p e) c -> p e c", e=2),
                )

        def load_small():
            nc.sync.dma_start(out=b1raw[:], in_=b1.rearrange("(p j) -> p j", j=PACK))
            nc.sync.dma_start(out=w2raw[:], in_=W2.rearrange("(p t) f -> p t f", t=PACK))
            nc.sync.dma_start(out=b2raw[:], in_=b2.rearrange("(p o) -> p o", o=1))

        def w1_group(copy, j):
            copy(
                out=w1g[:, j * P : (j + 1) * P, :],
                in_=w1raw[:].rearrange("p t (m j) -> p j m t", j=PACK)[:, j],
            )

        def w1_quant(j):
            nc.vector.quantize_mx(
                out=w1q[:, j * P : (j + 1) * P].bitcast(FP8X4),
                scales=w1s[:, j * P : (j + 1) * P],
                in_=w1g[:, j * P : (j + 1) * P, :].rearrange("p m t -> p (m t)"),
            )

        def w2_quant():
            nc.vector.quantize_mx(
                out=w2q[:].bitcast(FP8X4),
                scales=w2s[:],
                in_=w2g[:].rearrange("p f t -> p (f t)"),
            )

        def b2_spread():
            spread = ps_t.tile([P, CH], F32, name="ot")
            nc.tensor.matmul(
                spread[:, :F], b2f[:, 0:1].to_broadcast([P, P]), ident[:], start=True, stop=True
            )
            live["spread"] = spread

        def b2_copy():
            nc.scalar.copy(out=b2row[:], in_=live["spread"][:, :F])

        def load(c):
            w = WIDTHS[c]
            x_sb = xin.tile([P, w // P, D], BF16, name="x_sb")
            nc.sync.dma_start(
                out=x_sb[:],
                in_=x[ROW0[c] : ROW0[c] + w, :].rearrange("(p r) k -> p r k", r=w // P),
            )
            live["x", c] = x_sb

        def transposes(c):
            xw = live["x", c][:].bitcast(F32)
            tiles = WIDTHS[c] // P
            for i in range((tiles + 1) // 2):
                xt = ps_x.tile([P, 2, 2, P], F32, name="xt")
                for rr in range(min(2, tiles - 2 * i)):
                    for u in range(2):
                        nc.tensor.transpose(
                            xt[:, rr, u, :], xw[:, 2 * i + rr, u * P : (u + 1) * P], ident[:]
                        )
                live["xt", c, i] = xt

        def evacuate(c):
            xg = xgp.tile([P, WIDTHS[c] * PACK], BF16, align_bytes=64, name="xg")
            xg32 = xg[:].bitcast(F32)
            copy = nc.vector.tensor_copy if c == 1 else nc.scalar.copy
            tiles = WIDTHS[c] // P
            for i in range((tiles + 1) // 2):
                n = min(2, tiles - 2 * i)
                copy(
                    out=xg32[:, 512 * i : 512 * i + 256 * n].rearrange(
                        "p (r b u) -> p r b u", r=n, u=2
                    ),
                    in_=live["xt", c, i][:, :n].rearrange("p r u b -> p r b u"),
                )
            live["xg", c] = xg

        def quant_x(c):
            xq = xqp.tile([P, WIDTHS[c]], U32, align_bytes=64, name="xq")
            xs = xqp.tile([P, WIDTHS[c]], U8, align_bytes=64, name="xs")
            nc.vector.quantize_mx(out=xq[:].bitcast(FP8X4), scales=xs[:], in_=live["xg", c][:])
            live["xq", c] = xq
            live["xs", c] = xs

        def layer1(c, j):
            bank = ps_a.tile([P, CH], F32, name="a")
            a = bank[:, : WIDTHS[c]]
            nc.tensor.matmul_mx(
                out=a,
                lhsT=w1q[:, j * P : (j + 1) * P].bitcast(FP8X4),
                lhsT_scale=w1s[:, j * P : (j + 1) * P],
                rhs=live["xq", c][:].bitcast(FP8X4),
                rhs_scale=live["xs", c][:],
                start=True,
                stop=True,
            )
            live["a", c, j] = a

        def tanh(c, j):
            if j == 0:
                live["t", c] = act.tile([P, PACK, WIDTHS[c]], F32, name="t")
                live["u", c] = act.tile([P, PACK, WIDTHS[c]], F32, name="u_t")
                live["y", c] = act.tile([P, PACK, WIDTHS[c]], F32, name="y")
            nc.scalar.activation(
                out=live["t", c][:, j, :],
                in_=live["a", c, j],
                func=ACT.Tanh,
                bias=b1raw[:, j : j + 1],
                scale=1.0,
            )

        def mix(c, j):
            nc.vector.scalar_tensor_tensor(
                out=live["u", c][:, j, :],
                in0=live["t", c][:, j, :],
                scalar=1.0 / 9.0,
                in1=live["a", c, j],
                op0=ALU.mult,
                op1=ALU.add,
            )

        def affine_gpsimd(c, j):
            n = WIDTHS[c] * GP_SHARE[j] // 4
            if n > 0:
                nc.gpsimd.tensor_scalar(
                    out=live["y", c][:, j, :n],
                    in0=live["u", c][:, j, :n],
                    scalar1=1.8,
                    scalar2=b1s[:, j : j + 1],
                    op0=ALU.mult,
                    op1=ALU.add,
                )

        def affine_scalar(c, j):
            n = WIDTHS[c] * GP_SHARE[j] // 4
            if n < WIDTHS[c]:
                nc.scalar.activation(
                    out=live["y", c][:, j, n:],
                    in_=live["u", c][:, j, n:],
                    func=ACT.Identity,
                    bias=b1s[:, j : j + 1],
                    scale=1.8,
                )

        def blend_max(c):
            hg = hgp.tile([P, WIDTHS[c], PACK], BF16, align_bytes=64, name="hg")
            nc.vector.tensor_tensor(
                out=hg[:].rearrange("p (c i) j -> p c j i", i=4),
                in0=live["t", c][:].rearrange("p j (c i) -> p c j i", i=4),
                in1=live["y", c][:].rearrange("p j (c i) -> p c j i", i=4),
                op=ALU.max,
            )
            live["hg", c] = hg

        def quant_h(c):
            hq = hqp.tile([P, WIDTHS[c]], U32, align_bytes=64, name="hq")
            hs = hqp.tile([P, WIDTHS[c]], U8, align_bytes=64, name="hs")
            nc.vector.quantize_mx(
                out=hq[:].bitcast(FP8X4),
                scales=hs[:],
                in_=live["hg", c][:].rearrange("p n j -> p (n j)"),
            )
            live["hq", c] = hq
            live["hs", c] = hs

        def layer2(c):
            if c < NCH - 3:
                bank = ps_o.tile([P, CH], F32, name="o_ps")
            else:
                bank = ps_x.tile([P, CH], F32, name="xt")
            o_ps = bank[:, : WIDTHS[c]]
            nc.tensor.matmul_mx(
                out=o_ps,
                lhsT=w2q[:].bitcast(FP8X4),
                lhsT_scale=w2s[:],
                rhs=live["hq", c][:].bitcast(FP8X4),
                rhs_scale=live["hs", c][:],
                start=True,
                stop=True,
            )
            live["o_ps", c] = o_ps

        def bias_relu(c):
            o_t = outp.tile([P, WIDTHS[c]], F32, name="o_t")
            nc.scalar.activation(
                out=o_t[:], in_=live["o_ps", c], func=ACT.Relu, bias=b2raw[:, 0:1], scale=0.5
            )
            live["o_t", c] = o_t

        def turn_back(c):
            if c < NCH - 3:
                bank = ps_t.tile([P, CH], F32, name="ot")
            else:
                bank = ps_x.tile([P, CH], F32, name="xt")
            ot = bank[:, : WIDTHS[c]]
            for r in range(WIDTHS[c] // P):
                cols = slice(r * P, (r + 1) * P)
                nc.tensor.transpose(ot[:, cols], live["o_t", c][:, cols], ident[:])
            live["ot", c] = ot

        def store(c):
            o_sb = outp.tile([P, WIDTHS[c]], F32, name="o_sb")
            nc.scalar.copy(out=o_sb[:], in_=live["ot", c])
            nc.sync.dma_start(
                out=out[ROW0[c] : ROW0[c] + WIDTHS[c], :].rearrange(
                    "(p r) f -> p (r f)", r=WIDTHS[c] // P
                ),
                in_=o_sb[:],
            )

        def layer2_rows(c):
            bank = ps_a.tile([P, CH], F32, name="a")
            o_ps = bank[:, :F]
            nc.tensor.matmul_mx(
                out=o_ps,
                lhsT=live["hq", c][:].bitcast(FP8X4),
                lhsT_scale=live["hs", c][:],
                rhs=w2q[:].bitcast(FP8X4),
                rhs_scale=w2s[:],
                start=True,
                stop=True,
            )
            live["o_ps", c] = o_ps

        def bias_rows(c):
            o_t = outp.tile([P, F], F32, name="o_t")
            nc.vector.scalar_tensor_tensor(
                out=o_t[:],
                in0=live["o_ps", c],
                scalar=0.5,
                in1=b2row[:],
                op0=ALU.mult,
                op1=ALU.add,
            )
            live["o_t", c] = o_t

        def store_rows(c):
            o_sb = outp.tile([P, F], F32, name="o_sb")
            nc.vector.tensor_scalar_max(out=o_sb[:], in0=live["o_t", c][:], scalar1=0.0)
            nc.sync.dma_start(out=out[ROW0[c] : ROW0[c] + P, :], in_=o_sb[:])

        for s in range(-4, NCH - 1):
            if ok(s + 4):
                load(s + 4)
            if s == -3:
                load_small()
                nc.gpsimd.tensor_scalar(
                    out=w2g[:],
                    in0=w2raw[:].rearrange("p t f -> p f t"),
                    scalar1=1.0,
                    scalar2=0.0,
                    op0=ALU.mult,
                    op1=ALU.add,
                )
                nc.gpsimd.tensor_copy(out=b2f[:], in_=b2raw[:])
                nc.gpsimd.tensor_scalar(
                    out=b1s[:], in0=b1raw[:], scalar1=1.8, scalar2=0.0, op0=ALU.mult, op1=ALU.add
                )
            if s == -4:
                load_w1()
                w1_group(nc.vector.tensor_copy, 0)
                w1_group(nc.vector.tensor_copy, 1)
                w1_quant(0)
                w1_quant(1)
            if ok(s - 4):
                store(s - 4)
            if ok(s - 3):
                bias_relu(s - 3)
            if ok(s + 2):
                evacuate(s + 2)
            if s == -2:
                w1_group(nc.scalar.copy, 2)
                w1_group(nc.scalar.copy, 3)
            for j in range(PACK):
                if ok(s):
                    mix(s, j)
                    affine_gpsimd(s, j)
                if ok(s + 1):
                    layer1(s + 1, j)
            if s == 0:
                w2_quant()
            if ok(s):
                for j in range(PACK):
                    affine_scalar(s, j)
            for j in range(PACK):
                if ok(s + 1):
                    tanh(s + 1, j)
            if ok(s - 2):
                layer2(s - 2)
            if ok(s - 3):
                turn_back(s - 3)
            if ok(s + 3):
                transposes(s + 3)
            if s == -1:
                b2_spread()
            if s == 2:
                b2_copy()
            if ok(s - 1):
                blend_max(s - 1)
            if ok(s + 2):
                quant_x(s + 2)
            if s == -2:
                w1_quant(2)
                w1_quant(3)
            if ok(s - 1):
                quant_h(s - 1)

        end = NCH - 1
        store(end - 4)
        bias_relu(end - 3)
        for j in range(PACK):
            mix(end, j)
            affine_gpsimd(end, j)
        layer2(end - 2)
        turn_back(end - 3)
        bias_relu(end - 2)
        turn_back(end - 2)
        for j in range(PACK):
            affine_scalar(end, j)
        store(end - 3)
        store(end - 2)
        blend_max(end - 1)
        blend_max(end)
        quant_h(end - 1)
        quant_h(end)
        layer2_rows(end - 1)
        layer2_rows(end)
        bias_rows(end - 1)
        bias_rows(end)
        store_rows(end - 1)
        store_rows(end)
